import numpy as np
import ml_dtypes


def mxq(x, axis, fmt="e4m3"):
    dtype, down = {"e4m3": (ml_dtypes.float8_e4m3fn, 7), "e5m2": (ml_dtypes.float8_e5m2, 14)}[fmt]
    v = np.moveaxis(np.asarray(x, np.float32).astype(ml_dtypes.bfloat16).astype(np.float64), axis, -1)
    blocks = v.reshape(v.shape[:-1] + (-1, 32))
    amax = np.abs(blocks).max(-1, keepdims=True)
    byte = np.maximum(np.where(amax > 0, np.frexp(amax)[1] - 1 + 127, 0) - down, 1)
    scale = np.exp2(byte - 127.0)
    codes = (blocks / scale).astype(np.float32).astype(dtype).astype(np.float64)
    return np.moveaxis((codes * scale).reshape(v.shape), -1, axis)


WIDE = False


def mx_kscale(k):
    if not WIDE:
        return np.ones(k)
    levels = np.array([10, -10, 5, -5, 0])
    a = np.random.permutation(np.resize(levels, k // 512 * 4)).reshape(k // 512, 4)
    idx = np.arange(k)
    return np.exp2(a[idx // 512, idx % 128 // 32])


BF16 = ml_dtypes.bfloat16


def bf(x):
    return np.asarray(x, np.float32).astype(BF16)


def f64(x):
    return np.asarray(x).astype(np.float64)


E2M1 = np.array([0.0, 0.5, 1.0, 1.5, 2.0, 3.0, 4.0, 6.0, -0.0, -0.5, -1.0, -1.5, -2.0, -3.0, -4.0, -6.0])


def pack_weight(w, fmt):
    k, n = w.shape
    w = f64(bf(w)).reshape(k // 32, 32, n)
    amax = np.abs(w).max(1)
    if fmt == "e4m3":
        byte = np.frexp(amax)[1] - 1 + 127 - 7
    else:
        mant, ex = np.frexp(amax / 6.0)
        byte = np.where(mant > 0.5, ex, ex - 1) + 127
    byte = np.clip(np.where(amax > 0, byte, 1), 1, 254)
    scaled = (w * np.exp2(127.0 - byte)[:, None, :]).reshape(k, n).astype(np.float32)
    by_word = np.ascontiguousarray(scaled.reshape(k // 512, 128, 4, n).transpose(0, 1, 3, 2))
    if fmt == "e4m3":
        words = by_word.astype(ml_dtypes.float8_e4m3fn).view(np.uint8)
    else:
        c = by_word.astype(ml_dtypes.float4_e2m1fn).view(np.uint8) & 0xF
        words = c[..., 0::2] | (c[..., 1::2] << 4)
    return np.ascontiguousarray(words), np.ascontiguousarray(byte.astype(np.uint8).reshape(k // 512, 16, n))


def unpack_weight(words, scales, fmt):
    g, p, n, _ = words.shape
    if fmt == "e4m3":
        vals = np.ascontiguousarray(words).view(ml_dtypes.float8_e4m3fn).astype(np.float64)
    else:
        nib = np.empty((g, p, n, 4), np.uint8)
        nib[..., 0::2] = words & 0xF
        nib[..., 1::2] = words >> 4
        vals = E2M1[nib]
    vals = vals * np.repeat(np.exp2(scales.astype(np.float64) - 127.0), 8, axis=1)[..., None]
    return vals.transpose(0, 1, 3, 2).reshape(g * 512, n)


B, In, H, Hh, E, G = 256, 8192, 512, 256, 128, 4
EPS = 1e-6


def rn(*shape):
    return np.random.standard_normal(shape)


def sigmoid(v):
    return 1.0 / (1.0 + np.exp(-v))


def ln(a, gamma, beta):
    mean = a.mean(-1, keepdims=True)
    std = a.std(-1, keepdims=True, ddof=1)
    return gamma * (a - mean) / (std + EPS) + beta


def expand(emb, w):
    return (emb.transpose(1, 0, 2) @ w.transpose(0, 2, 1)).transpose(1, 0, 2)


def setup_inputs():
    s, t = mx_kscale(In), mx_kscale(H)
    x = bf(rn(B, In) * s)
    h = bf(rn(B, H) * t)
    c = bf(rn(B, H))
    emb_h = bf(1.0 + 0.5 * rn(B, G, E))
    emb_x = bf(1.0 + 0.5 * rn(B, G, E))
    emb_b = bf(rn(B, G, E))
    Wsh = bf(1.0 / E + 0.5 * rn(G, H, E) / np.sqrt(E))
    Wsx = bf(1.0 / E + 0.5 * rn(G, H, E) / np.sqrt(E))
    Wsb = bf(0.5 * rn(G, H, E) / np.sqrt(E))
    Wih_words, Wih_scales = pack_weight((rn(G * H, In) / np.sqrt(In) / s[None, :]).T, 'e4m3')
    Whh_words, Whh_scales = pack_weight((rn(G * H, H) / np.sqrt(H) / t[None, :]).T, 'e4m3')
    bias = bf(0.3 * rn(G * H))
    ln_gamma = bf(1.0 + 0.1 * rn(G, H))
    ln_beta = bf(0.1 * rn(G, H))
    lnc_gamma = bf(1.0 + 0.1 * rn(H))
    lnc_beta = bf(0.1 * rn(H))
    return {
        'x': x,
        'h': h,
        'c': c,
        'emb_h': emb_h,
        'emb_x': emb_x,
        'emb_b': emb_b,
        'Wsh': Wsh,
        'Wsx': Wsx,
        'Wsb': Wsb,
        'Wih_words': Wih_words,
        'Wih_scales': Wih_scales,
        'Whh_words': Whh_words,
        'Whh_scales': Whh_scales,
        'bias': bias,
        'ln_gamma': ln_gamma,
        'ln_beta': ln_beta,
        'lnc_gamma': lnc_gamma,
        'lnc_beta': lnc_beta,
    }


def reference(x, h, c, emb_h, emb_x, emb_b, Wsh, Wsx, Wsb, Wih_words, Wih_scales, Whh_words, Whh_scales, bias, ln_gamma, ln_beta, lnc_gamma, lnc_beta):
    zh = expand(f64(emb_h), f64(Wsh))
    zx = expand(f64(emb_x), f64(Wsx))
    zb = expand(f64(emb_b), f64(Wsb))
    xh = (mxq(f64(x), 1, 'e4m3') @ unpack_weight(Wih_words, Wih_scales, 'e4m3')).reshape(B, G, H)
    hh = (mxq(f64(h), 1, 'e4m3') @ unpack_weight(Whh_words, Whh_scales, 'e4m3')).reshape(B, G, H)
    gates = xh * zx + hh * zh + (f64(bias).reshape(G, H) + zb)
    gates = ln(gates, f64(ln_gamma), f64(ln_beta))
    i, f, g, o = gates[:, 0], gates[:, 1], gates[:, 2], gates[:, 3]
    new_c = f64(c) * sigmoid(f) + sigmoid(i) * np.tanh(g)
    new_c = ln(new_c, f64(lnc_gamma), f64(lnc_beta))
    new_h = np.tanh(new_c) * sigmoid(o)
    return new_h, new_c

@@ -1,0 +1,376 @@
+import math
+from contextlib import ExitStack
+
+import concourse.mybir as mybir
+from concourse.masks import make_identity
+
+F32 = mybir.dt.float32
+BF16 = mybir.dt.bfloat16
+I32 = mybir.dt.int32
+U32 = mybir.dt.uint32
+U8 = mybir.dt.uint8
+FP8X4 = mybir.dt.float8_e4m3fn_x4
+ALU = mybir.AluOpType
+ACT = mybir.ActivationFunctionType
+
+P = 128
+BATCH, IN, H, E, GATES = 256, 8192, 512, 128, 4
+M_TILES = BATCH // P
+PACK = 4
+K_PASS = P * PACK
+X_PASSES = IN // K_PASS
+PASSES_PER_CHUNK = 4
+CHUNKS = X_PASSES // PASSES_PER_CHUNK
+RING = 8
+EPS = 1e-6
+GATE_I, GATE_F, GATE_G, GATE_O = 0, 1, 2, 3
+
+FLOPS = 2 * BATCH * (IN + H) * GATES * H + 3 * 2 * BATCH * GATES * H * E
+
+ROW_GAMMA, ROW_BETA, ROW_BIAS, ROW_CELL_GAMMA, ROW_CELL_BETA = 0, 4, 8, 12, 13
+ROWS = 14
+
+
+def units_in_order(ap):
+    return ap.rearrange("b (t q) -> b q t", t=PACK)
+
+
+def units_as_pairs(ap):
+    return ap.rearrange("b (q t) -> b q t", t=PACK)
+
+
+def transpose_and_quantise(nc, psum, grouped, words, passes, ident_f32, codes, scales):
+    for g in range(passes):
+        flipped = psum.tile([P, M_TILES, 2, P], F32, tag="work")
+        for m in range(M_TILES):
+            for u in range(2):
+                nc.tensor.transpose(
+                    flipped[:, m, u, :],
+                    words[m][:, 2 * P * g + u : 2 * P * (g + 1) : 2],
+                    ident_f32[:],
+                )
+        side_by_side = (
+            grouped[:, g]
+            .rearrange("p c t -> p (c t)")
+            .bitcast(F32)
+            .rearrange("p (m b u) -> p m b u", m=M_TILES, u=2)
+        )
+        if g % 2 == 0:
+            nc.vector.tensor_copy(out=side_by_side, in_=flipped[:].rearrange("p m u b -> p m b u"))
+        else:
+            nc.scalar.copy(out=side_by_side, in_=flipped[:].rearrange("p m u b -> p m b u"))
+    nc.vector.quantize_mx(
+        out=codes.rearrange("p g c -> p (g c)").bitcast(FP8X4),
+        scales=scales.rearrange("p g c -> p (g c)"),
+        in_=grouped[:].rearrange("p g c t -> p (g c t)"),
+    )
+
+
+def layer_norm(nc, work, stat, half, values, total, gamma, beta, out):
+    mean = stat.tile([P, 1], F32, tag="mean")
+    nc.vector.tensor_scalar(out=mean[:], in0=total[:], scalar1=1.0 / H, scalar2=None, op0=ALU.mult)
+    shift = stat.tile([P, 1], F32, tag="shift")
+    root = math.sqrt(H - 1)
+    nc.vector.tensor_scalar(out=shift[:], in0=total[:], scalar1=-1.0 / (H * root), scalar2=None, op0=ALU.mult)
+    squares = work.tile([P, H], F32, tag="squares")
+    variance = stat.tile([P, 1], F32, tag="variance")
+    nc.scalar.activation(
+        out=squares[:], in_=values, func=ACT.Square, bias=shift[:], scale=1.0 / root, accum_out=variance[:]
+    )
+    centred = work.tile([P, H], F32, tag="centred")
+    nc.vector.scalar_tensor_tensor(
+        out=centred[:], in0=values, scalar=mean[:], in1=gamma, op0=ALU.subtract, op1=ALU.mult
+    )
+    std = stat.tile([P, 1], F32, tag="std")
+    nc.gpsimd.tensor_tensor(out=std[:], in0=variance[:], in1=half[:], op=ALU.pow)
+    inverse = stat.tile([P, 1], F32, tag="inverse")
+    nc.vector.tensor_scalar(out=inverse[:], in0=std[:], scalar1=EPS, scalar2=None, op0=ALU.add)
+    nc.vector.reciprocal(out=inverse[:], in_=inverse[:])
+    nc.vector.scalar_tensor_tensor(out=out, in0=centred[:], scalar=inverse[:], in1=beta, op0=ALU.mult, op1=ALU.add)
+
+
+def tile_hyperlstmcell_pb_k_kernel(
+    tc,
+    x,
+    h,
+    c,
+    emb_h,
+    emb_x,
+    emb_b,
+    Wsh,
+    Wsx,
+    Wsb,
+    Wih_words,
+    Wih_scales,
+    Whh_words,
+    Whh_scales,
+    bias,
+    ln_gamma,
+    ln_beta,
+    lnc_gamma,
+    lnc_beta,
+    out_0,
+    out_1,
+):
+    nc = tc.nc
+    with ExitStack() as ctx:
+        keep = ctx.enter_context(tc.tile_pool(name="keep", bufs=1))
+        ring = ctx.enter_context(tc.tile_pool(name="ring", bufs=RING))
+        stat = ctx.enter_context(tc.tile_pool(name="stat", bufs=4))
+        sums = ctx.enter_context(tc.psum_pool(name="sums", bufs=4))
+        psum = ctx.enter_context(tc.psum_pool(name="psum", bufs=4))
+
+        ident_f32 = keep.tile([P, P], F32)
+        make_identity(nc, ident_f32[:])
+        ident_bf16 = keep.tile([P, P], BF16)
+        make_identity(nc, ident_bf16[:])
+        half = keep.tile([P, 1], F32)
+        nc.vector.memset(half[:], 0.5)
+        warm = keep.tile([P, 1], F32)
+        nc.scalar.activation(out=warm[:], in_=half[:], func=ACT.Sigmoid)
+
+        rows = keep.tile([P, H], BF16)
+        nc.vector.memset(rows[:], 0.0)
+        nc.scalar.dma_start(out=rows[ROW_GAMMA : ROW_GAMMA + GATES, :], in_=ln_gamma)
+        nc.scalar.dma_start(out=rows[ROW_BETA : ROW_BETA + GATES, :], in_=ln_beta)
+        nc.scalar.dma_start(out=rows[ROW_BIAS : ROW_BIAS + GATES, :], in_=bias.rearrange("(g n) -> g n", g=GATES))
+        nc.scalar.dma_start(out=rows[ROW_CELL_GAMMA : ROW_CELL_GAMMA + 1, :], in_=lnc_gamma.rearrange("(o n) -> o n", o=1))
+        nc.scalar.dma_start(out=rows[ROW_CELL_BETA : ROW_CELL_BETA + 1, :], in_=lnc_beta.rearrange("(o n) -> o n", o=1))
+
+        planes = keep.tile([P, CHUNKS + 1, GATES * H], U8, align_bytes=64)
+        nc.vector.memset(planes[:].rearrange("p j n -> p (j n)").bitcast(I32), 0)
+
+        with tc.tile_pool(name="raw", bufs=1) as raw:
+            x_by_tile = x.rearrange("(m p) k -> p m k", p=P)
+            x_cols = PASSES_PER_CHUNK * K_PASS
+            x_raw = []
+            for j in range(CHUNKS):
+                x_chunk = raw.tile([P, M_TILES, x_cols], BF16, name="x_raw%d" % j)
+                nc.sync.dma_start(out=x_chunk[:], in_=x_by_tile[:, :, j * x_cols : (j + 1) * x_cols])
+                x_raw.append(x_chunk)
+            h_raw = raw.tile([P, M_TILES, H], BF16)
+            nc.sync.dma_start(out=h_raw[:], in_=h.rearrange("(m p) k -> p m k", p=P))
+            emb_raw = {}
+            ws_raw = {}
+            for which, emb in (("x", emb_x), ("h", emb_h), ("b", emb_b)):
+                emb_raw[which] = raw.tile([P, M_TILES, GATES * E], BF16, name="emb_raw_" + which)
+                nc.sync.dma_start(out=emb_raw[which][:], in_=emb.rearrange("(m p) g e -> p m (g e)", p=P))
+            for which, ws in (("x", Wsx), ("h", Wsh), ("b", Wsb)):
+                ws_raw[which] = raw.tile([P, GATES, PACK, E], BF16, name="ws_raw_" + which)
+                nc.sync.dma_start(
+                    out=ws_raw[which][:].rearrange("q g t e -> q g (t e)"),
+                    in_=ws.rearrange("g (q t) e -> q g (t e)", t=PACK),
+                )
+            c_raw = keep.tile([P, M_TILES, H], BF16)
+            nc.sync.dma_start(out=c_raw[:], in_=c.rearrange("(m p) k -> p m k", p=P))
+
+            for quad in range(4):
+                nc.sync.dma_start(
+                    out=planes[32 * quad : 32 * quad + 4, CHUNKS, :].bitcast(I32),
+                    in_=Whh_scales[0, 4 * quad : 4 * quad + 4, :].bitcast(I32),
+                )
+            for j in range(CHUNKS):
+                for quad in range(4):
+                    nc.sync.dma_start(
+                        out=planes[32 * quad : 32 * quad + 16, j, :].bitcast(I32),
+                        in_=Wih_scales[
+                            PASSES_PER_CHUNK * j : PASSES_PER_CHUNK * (j + 1), 4 * quad : 4 * quad + 4, :
+                        ].bitcast(I32),
+                    )
+            whh = keep.tile([P, GATES * H * PACK], U8, align_bytes=64)
+            nc.sync.dma_start(out=whh[:].bitcast(I32), in_=Whh_words[0].rearrange("p n t -> p (n t)").bitcast(I32))
+
+            wih_bytes = Wih_words.rearrange("g p n t -> p g (n t)")
+            w_chunks = {}
+
+            def load_weights(index):
+                gate, j = divmod(index, CHUNKS)
+                chunk = ring.tile([P, PASSES_PER_CHUNK, H * PACK], U8, tag="w", name="w%d" % index, align_bytes=64)
+                nc.sync.dma_start(
+                    out=chunk[:].bitcast(I32),
+                    in_=wih_bytes[
+                        :,
+                        PASSES_PER_CHUNK * j : PASSES_PER_CHUNK * (j + 1),
+                        gate * H * PACK : (gate + 1) * H * PACK,
+                    ].bitcast(I32),
+                )
+                w_chunks[index] = chunk
+
+            for index in range(RING):
+                load_weights(index)
+
+            spread = keep.tile([P, ROWS, H], BF16)
+            for r in range(0, ROWS, 2):
+                both = psum.tile([P, 2, H], BF16, tag="work")
+                for i in range(2):
+                    nc.tensor.matmul(
+                        both[:, i, :],
+                        lhsT=ident_bf16[:, r + i : r + i + 1].to_broadcast([P, P]),
+                        rhs=rows[:],
+                        start=True,
+                        stop=True,
+                    )
+                nc.scalar.copy(out=spread[:, r : r + 2, :], in_=both[:])
+
+            x_codes = keep.tile([P, X_PASSES, BATCH], U32, align_bytes=64)
+            x_scales = keep.tile([P, X_PASSES, BATCH], U8, align_bytes=64)
+            for j in range(CHUNKS):
+                grouped = raw.tile([P, PASSES_PER_CHUNK, BATCH, PACK], BF16, tag="grouped", bufs=2, align_bytes=64)
+                these = slice(PASSES_PER_CHUNK * j, PASSES_PER_CHUNK * (j + 1))
+                transpose_and_quantise(
+                    nc,
+                    psum,
+                    grouped,
+                    [x_raw[j][:, m, :].bitcast(F32) for m in range(M_TILES)],
+                    PASSES_PER_CHUNK,
+                    ident_f32,
+                    x_codes[:, these, :],
+                    x_scales[:, these, :],
+                )
+            h_codes = keep.tile([P, 1, BATCH], U32, align_bytes=64)
+            h_scales = keep.tile([P, 1, BATCH], U8, align_bytes=64)
+            h_grouped = raw.tile([P, 1, BATCH, PACK], BF16, align_bytes=64)
+            transpose_and_quantise(
+                nc,
+                psum,
+                h_grouped,
+                [h_raw[:, m, :].bitcast(F32) for m in range(M_TILES)],
+                1,
+                ident_f32,
+                h_codes[:],
+                h_scales[:],
+            )
+
+            emb_t = {}
+            ws_t = {}
+            for which in ("x", "h", "b"):
+                emb_t[which] = keep.tile([P, GATES, BATCH], BF16, name="emb_t_" + which)
+                for first in range(0, GATES, 2):
+                    flipped = psum.tile([P, 2, M_TILES, P], BF16, tag="work")
+                    for i in range(2):
+                        for m in range(M_TILES):
+                            nc.tensor.transpose(
+                                flipped[:, i, m, :],
+                                emb_raw[which][:, m, (first + i) * E : (first + i + 1) * E],
+                                ident_bf16[:],
+                            )
+                    nc.scalar.copy(
+                        out=emb_t[which][:, first : first + 2, :].rearrange("e g b -> e (g b)"),
+                        in_=flipped[:].rearrange("e g m b -> e (g m b)"),
+                    )
+                ws_t[which] = keep.tile([P, GATES, H], BF16, name="ws_t_" + which)
+                for gate in range(GATES):
+                    flipped = psum.tile([P, PACK, P], BF16, tag="work")
+                    for t in range(PACK):
+                        nc.tensor.transpose(flipped[:, t, :], ws_raw[which][:, gate, t, :], ident_bf16[:])
+                    nc.scalar.copy(out=ws_t[which][:, gate, :], in_=flipped[:].rearrange("e t q -> e (t q)"))
+
+        with tc.tile_pool(name="late", bufs=1, reuse_waits="tile") as late, tc.tile_pool(name="work", bufs=2, reuse_waits="tile") as work:
+            tiles = [(gate, m) for gate in range(GATES) for m in range(M_TILES)]
+
+            def expand(which, gate, m):
+                z = psum.tile([P, H], F32, tag="work")
+                nc.tensor.matmul(
+                    z[:],
+                    lhsT=emb_t[which][:, gate, m * P : (m + 1) * P],
+                    rhs=ws_t[which][:, gate, :],
+                    start=True,
+                    stop=True,
+                )
+                return z
+
+            zx = {}
+            zh = {}
+            rest = {}
+            for gate, m in tiles:
+                zx[gate, m] = late.tile([P, H], F32, name="zx%d_%d" % (gate, m))
+                nc.scalar.copy(out=units_as_pairs(zx[gate, m][:]), in_=units_in_order(expand("x", gate, m)[:]))
+                zh[gate, m] = late.tile([P, H], F32, name="zh%d_%d" % (gate, m))
+                nc.scalar.copy(out=units_as_pairs(zh[gate, m][:]), in_=units_in_order(expand("h", gate, m)[:]))
+                rest[gate, m] = late.tile([P, H], F32, name="rest%d_%d" % (gate, m))
+                nc.vector.tensor_tensor(
+                    out=units_as_pairs(rest[gate, m][:]),
+                    in0=units_in_order(expand("b", gate, m)[:]),
+                    in1=units_as_pairs(spread[:, ROW_BIAS + gate, :]),
+                    op=ALU.add,
+                )
+            for gate, m in tiles:
+                hh = psum.tile([P, H], F32, tag="work")
+                nc.tensor.matmul_mx(
+                    out=hh[:],
+                    lhsT=h_codes[:, 0, m * P : (m + 1) * P].bitcast(FP8X4),
+                    lhsT_scale=h_scales[:, 0, m * P : (m + 1) * P],
+                    rhs=whh[:, gate * H * PACK : (gate + 1) * H * PACK].bitcast(FP8X4),
+                    rhs_scale=planes[:, CHUNKS, gate * H : (gate + 1) * H],
+                    start=True,
+                    stop=True,
+                )
+                nc.vector.tensor_tensor(out=zh[gate, m][:], in0=hh[:], in1=zh[gate, m][:], op=ALU.mult)
+                nc.vector.tensor_tensor(out=rest[gate, m][:], in0=rest[gate, m][:], in1=zh[gate, m][:], op=ALU.add)
+
+            squashed = {}
+            tanh_c = {}
+            for gate in range(GATES):
+                xh = [sums.tile([P, H], F32, tag="xh", name="xh%d_%d" % (gate, m)) for m in range(M_TILES)]
+                for j in range(CHUNKS):
+                    index = gate * CHUNKS + j
+                    for i in range(PASSES_PER_CHUNK):
+                        g = PASSES_PER_CHUNK * j + i
+                        for m in range(M_TILES):
+                            nc.tensor.matmul_mx(
+                                out=xh[m][:],
+                                lhsT=x_codes[:, g, m * P : (m + 1) * P].bitcast(FP8X4),
+                                lhsT_scale=x_scales[:, g, m * P : (m + 1) * P],
+                                rhs=w_chunks[index][:, i, :].bitcast(FP8X4),
+                                rhs_scale=planes[4 * i : P, j, gate * H : (gate + 1) * H],
+                                start=(g == 0),
+                                stop=(g == X_PASSES - 1),
+                            )
+                    if index + RING < GATES * CHUNKS:
+                        load_weights(index + RING)
+
+                for m in range(M_TILES):
+                    pre = work.tile([P, H], F32, tag="pre")
+                    nc.vector.tensor_tensor(out=pre[:], in0=xh[m][:], in1=zx[gate, m][:], op=ALU.mult)
+                    total = stat.tile([P, 1], F32, tag="total")
+                    nc.vector.scalar_tensor_tensor(
+                        out=pre[:], in0=pre[:], scalar=1.0, in1=rest[gate, m][:], op0=ALU.mult, op1=ALU.add,
+                        accum_out=total[:],
+                    )
+                    normed = work.tile([P, H], F32, tag="normed")
+                    layer_norm(
+                        nc, work, stat, half, pre[:], total,
+                        spread[:, ROW_GAMMA + gate, :], spread[:, ROW_BETA + gate, :], normed[:],
+                    )
+                    squashed[gate, m] = late.tile([P, H], F32, name="squashed%d_%d" % (gate, m))
+                    nc.scalar.activation(
+                        out=squashed[gate, m][:], in_=normed[:], func=(ACT.Tanh if gate == GATE_G else ACT.Sigmoid)
+                    )
+
+                if gate == GATE_F:
+                    for m in range(M_TILES):
+                        nc.vector.tensor_tensor(
+                            out=squashed[GATE_F, m][:], in0=squashed[GATE_F, m][:], in1=c_raw[:, m, :], op=ALU.mult
+                        )
+                if gate == GATE_G:
+                    for m in range(M_TILES):
+                        nc.vector.tensor_tensor(
+                            out=squashed[GATE_I, m][:], in0=squashed[GATE_I, m][:], in1=squashed[GATE_G, m][:], op=ALU.mult
+                        )
+                        total = stat.tile([P, 1], F32, tag="total")
+                        nc.vector.scalar_tensor_tensor(
+                            out=squashed[GATE_I, m][:], in0=squashed[GATE_I, m][:], scalar=1.0, in1=squashed[GATE_F, m][:],
+                            op0=ALU.mult, op1=ALU.add, accum_out=total[:],
+                        )
+                        new_c = late.tile([P, H], F32, name="new_c%d" % m)
+                        layer_norm(
+                            nc, work, stat, half, squashed[GATE_I, m][:], total,
+                            spread[:, ROW_CELL_GAMMA, :], spread[:, ROW_CELL_BETA, :], new_c[:],
+                        )
+                        nc.sync.dma_start(out=out_1[m * P : (m + 1) * P, :], in_=new_c[:])
+                        tanh_c[m] = late.tile([P, H], F32, name="tanh_c%d" % m)
+                        nc.scalar.activation(out=tanh_c[m][:], in_=new_c[:], func=ACT.Tanh)
+                if gate == GATE_O:
+                    for m in range(M_TILES):
+                        nc.vector.tensor_tensor(out=tanh_c[m][:], in0=tanh_c[m][:], in1=squashed[GATE_O, m][:], op=ALU.mult)
+                        nc.sync.dma_start(out=out_0[m * P : (m + 1) * P, :], in_=tanh_c[m][:])

@@ -15,15 +15,19 @@ ACT = mybir.ActivationFunctionType
 
 P = 128
 BATCH, IN, H, E, GATES = 256, 8192, 512, 128, 4
+GATE_I, GATE_F, GATE_G, GATE_O = 0, 1, 2, 3
 M_TILES = BATCH // P
 PACK = 4
 K_PASS = P * PACK
 X_PASSES = IN // K_PASS
-PASSES_PER_CHUNK = 4
-CHUNKS = X_PASSES // PASSES_PER_CHUNK
+PLANES_PER_TILE = 4
+PLANE_TILES = X_PASSES // PLANES_PER_TILE
+X_CHUNKS = 4
+PASSES_PER_CHUNK = X_PASSES // X_CHUNKS
+W_TILES_PER_GATE = PLANE_TILES
+PASSES_PER_LOAD = 2
 RING = 8
 EPS = 1e-6
-GATE_I, GATE_F, GATE_G, GATE_O = 0, 1, 2, 3
 
 FLOPS = 2 * BATCH * (IN + H) * GATES * H + 3 * 2 * BATCH * GATES * H * E
 
@@ -39,26 +43,16 @@ def units_as_pairs(ap):
     return ap.rearrange("b (q t) -> b q t", t=PACK)
 
 
-def transpose_and_quantise(nc, psum, grouped, words, passes, ident_f32, codes, scales):
-    for g in range(passes):
-        flipped = psum.tile([P, M_TILES, 2, P], F32, tag="work")
-        for m in range(M_TILES):
-            for u in range(2):
-                nc.tensor.transpose(
-                    flipped[:, m, u, :],
-                    words[m][:, 2 * P * g + u : 2 * P * (g + 1) : 2],
-                    ident_f32[:],
-                )
-        side_by_side = (
-            grouped[:, g]
-            .rearrange("p c t -> p (c t)")
-            .bitcast(F32)
-            .rearrange("p (m b u) -> p m b u", m=M_TILES, u=2)
-        )
-        if g % 2 == 0:
-            nc.vector.tensor_copy(out=side_by_side, in_=flipped[:].rearrange("p m u b -> p m b u"))
-        else:
-            nc.scalar.copy(out=side_by_side, in_=flipped[:].rearrange("p m u b -> p m b u"))
+def flip_pass(nc, banks, words, g, ident_f32, grouped, engine_copy):
+    flipped = banks.tile([P, M_TILES, 2, P], F32, tag="bank")
+    for m in range(M_TILES):
+        for u in range(2):
+            nc.tensor.transpose(flipped[:, m, u, :], words[m][:, 2 * P * g + u : 2 * P * (g + 1) : 2], ident_f32[:])
+    side_by_side = grouped.rearrange("p c t -> p (c t)").bitcast(F32).rearrange("p (m b u) -> p m b u", m=M_TILES, u=2)
+    engine_copy(out=side_by_side, in_=flipped[:].rearrange("p m u b -> p m b u"))
+
+
+def quantise(nc, grouped, codes, scales):
     nc.vector.quantize_mx(
         out=codes.rearrange("p g c -> p (g c)").bitcast(FP8X4),
         scales=scales.rearrange("p g c -> p (g c)"),
@@ -66,25 +60,24 @@ def transpose_and_quantise(nc, psum, grouped, words, passes, ident_f32, codes, s
     )
 
 
-def layer_norm(nc, work, stat, half, values, total, gamma, beta, out):
-    mean = stat.tile([P, 1], F32, tag="mean")
-    nc.vector.tensor_scalar(out=mean[:], in0=total[:], scalar1=1.0 / H, scalar2=None, op0=ALU.mult)
-    shift = stat.tile([P, 1], F32, tag="shift")
-    root = math.sqrt(H - 1)
-    nc.vector.tensor_scalar(out=shift[:], in0=total[:], scalar1=-1.0 / (H * root), scalar2=None, op0=ALU.mult)
+def norm_first_half(nc, work, stat, half, values, total, gamma):
+    minus_mean = stat.tile([P, 1], F32, tag="minus_mean")
+    nc.vector.tensor_scalar(out=minus_mean[:], in0=total[:], scalar1=-1.0 / H, scalar2=None, op0=ALU.mult)
     squares = work.tile([P, H], F32, tag="squares")
-    variance = stat.tile([P, 1], F32, tag="variance")
-    nc.scalar.activation(
-        out=squares[:], in_=values, func=ACT.Square, bias=shift[:], scale=1.0 / root, accum_out=variance[:]
-    )
+    sum_of_squares = stat.tile([P, 1], F32, tag="sum_of_squares")
+    nc.scalar.activation(out=squares[:], in_=values, func=ACT.Square, bias=minus_mean[:], accum_out=sum_of_squares[:])
     centred = work.tile([P, H], F32, tag="centred")
-    nc.vector.scalar_tensor_tensor(
-        out=centred[:], in0=values, scalar=mean[:], in1=gamma, op0=ALU.subtract, op1=ALU.mult
-    )
-    std = stat.tile([P, 1], F32, tag="std")
-    nc.gpsimd.tensor_tensor(out=std[:], in0=variance[:], in1=half[:], op=ALU.pow)
+    nc.vector.scalar_tensor_tensor(out=centred[:], in0=values, scalar=minus_mean[:], in1=gamma, op0=ALU.add, op1=ALU.mult)
+    root = stat.tile([P, 1], F32, tag="root")
+    nc.gpsimd.tensor_tensor(out=root[:], in0=sum_of_squares[:], in1=half[:], op=ALU.pow)
+    return centred, root
+
+
+def norm_second_half(nc, stat, centred, root, beta, out):
     inverse = stat.tile([P, 1], F32, tag="inverse")
-    nc.vector.tensor_scalar(out=inverse[:], in0=std[:], scalar1=EPS, scalar2=None, op0=ALU.add)
+    nc.vector.tensor_scalar(
+        out=inverse[:], in0=root[:], scalar1=1.0 / math.sqrt(H - 1), scalar2=EPS, op0=ALU.mult, op1=ALU.add
+    )
     nc.vector.reciprocal(out=inverse[:], in_=inverse[:])
     nc.vector.scalar_tensor_tensor(out=out, in0=centred[:], scalar=inverse[:], in1=beta, op0=ALU.mult, op1=ALU.add)
 
@@ -113,95 +106,92 @@ def tile_hyperlstmcell_pb_k_kernel(
     out_1,
 ):
     nc = tc.nc
+    batch_tiles = range(M_TILES)
     with ExitStack() as ctx:
+        ctx.enter_context(tc.manual_schedule())
         keep = ctx.enter_context(tc.tile_pool(name="keep", bufs=1))
         ring = ctx.enter_context(tc.tile_pool(name="ring", bufs=RING))
         stat = ctx.enter_context(tc.tile_pool(name="stat", bufs=4))
-        sums = ctx.enter_context(tc.psum_pool(name="sums", bufs=4))
-        psum = ctx.enter_context(tc.psum_pool(name="psum", bufs=4))
+        late = ctx.enter_context(tc.tile_pool(name="late", bufs=1))
+        banks = ctx.enter_context(tc.psum_pool(name="banks", bufs=8))
 
-        ident_f32 = keep.tile([P, P], F32)
-        make_identity(nc, ident_f32[:])
-        ident_bf16 = keep.tile([P, P], BF16)
-        make_identity(nc, ident_bf16[:])
+        rows = keep.tile([P, H], BF16)
+        nc.vector.memset(rows[:].bitcast(I32), 0)
         half = keep.tile([P, 1], F32)
         nc.vector.memset(half[:], 0.5)
+        ident_bf16 = keep.tile([P, P], BF16)
+        make_identity(nc, ident_bf16[:])
+        ident_f32 = keep.tile([P, P], F32)
+        make_identity(nc, ident_f32[:])
         warm = keep.tile([P, 1], F32)
         nc.scalar.activation(out=warm[:], in_=half[:], func=ACT.Sigmoid)
 
-        rows = keep.tile([P, H], BF16)
-        nc.vector.memset(rows[:], 0.0)
-        nc.scalar.dma_start(out=rows[ROW_GAMMA : ROW_GAMMA + GATES, :], in_=ln_gamma)
-        nc.scalar.dma_start(out=rows[ROW_BETA : ROW_BETA + GATES, :], in_=ln_beta)
-        nc.scalar.dma_start(out=rows[ROW_BIAS : ROW_BIAS + GATES, :], in_=bias.rearrange("(g n) -> g n", g=GATES))
-        nc.scalar.dma_start(out=rows[ROW_CELL_GAMMA : ROW_CELL_GAMMA + 1, :], in_=lnc_gamma.rearrange("(o n) -> o n", o=1))
-        nc.scalar.dma_start(out=rows[ROW_CELL_BETA : ROW_CELL_BETA + 1, :], in_=lnc_beta.rearrange("(o n) -> o n", o=1))
-
-        planes = keep.tile([P, CHUNKS + 1, GATES * H], U8, align_bytes=64)
+        planes = keep.tile([P, PLANE_TILES + 1, GATES * H], U8, align_bytes=64)
         nc.vector.memset(planes[:].rearrange("p j n -> p (j n)").bitcast(I32), 0)
 
         with tc.tile_pool(name="raw", bufs=1) as raw:
-            x_by_tile = x.rearrange("(m p) k -> p m k", p=P)
-            x_cols = PASSES_PER_CHUNK * K_PASS
-            x_raw = []
-            for j in range(CHUNKS):
-                x_chunk = raw.tile([P, M_TILES, x_cols], BF16, name="x_raw%d" % j)
-                nc.sync.dma_start(out=x_chunk[:], in_=x_by_tile[:, :, j * x_cols : (j + 1) * x_cols])
-                x_raw.append(x_chunk)
-            h_raw = raw.tile([P, M_TILES, H], BF16)
-            nc.sync.dma_start(out=h_raw[:], in_=h.rearrange("(m p) k -> p m k", p=P))
+            nc.sync.dma_start(out=rows[ROW_GAMMA : ROW_GAMMA + GATES, :], in_=ln_gamma)
+            nc.sync.dma_start(out=rows[ROW_BETA : ROW_BETA + GATES, :], in_=ln_beta)
+            nc.sync.dma_start(out=rows[ROW_BIAS : ROW_BIAS + GATES, :], in_=bias.rearrange("(g n) -> g n", g=GATES))
+            nc.sync.dma_start(out=rows[ROW_CELL_GAMMA : ROW_CELL_GAMMA + 1, :], in_=lnc_gamma.rearrange("(o n) -> o n", o=1))
+            nc.sync.dma_start(out=rows[ROW_CELL_BETA : ROW_CELL_BETA + 1, :], in_=lnc_beta.rearrange("(o n) -> o n", o=1))
             emb_raw = {}
             ws_raw = {}
-            for which, emb in (("x", emb_x), ("h", emb_h), ("b", emb_b)):
+            for which, emb, ws in (("x", emb_x, Wsx), ("h", emb_h, Wsh), ("b", emb_b, Wsb)):
                 emb_raw[which] = raw.tile([P, M_TILES, GATES * E], BF16, name="emb_raw_" + which)
                 nc.sync.dma_start(out=emb_raw[which][:], in_=emb.rearrange("(m p) g e -> p m (g e)", p=P))
-            for which, ws in (("x", Wsx), ("h", Wsh), ("b", Wsb)):
                 ws_raw[which] = raw.tile([P, GATES, PACK, E], BF16, name="ws_raw_" + which)
                 nc.sync.dma_start(
                     out=ws_raw[which][:].rearrange("q g t e -> q g (t e)"),
                     in_=ws.rearrange("g (q t) e -> q g (t e)", t=PACK),
                 )
-            c_raw = keep.tile([P, M_TILES, H], BF16)
-            nc.sync.dma_start(out=c_raw[:], in_=c.rearrange("(m p) k -> p m k", p=P))
-
+            x_by_tile = x.rearrange("(m p) k -> p m k", p=P)
+            x_cols = PASSES_PER_CHUNK * K_PASS
+            x_raw = []
+            for j in range(X_CHUNKS):
+                x_chunk = ring.tile([P, M_TILES, x_cols], BF16, tag="slot", name="x_raw%d" % j, align_bytes=64)
+                nc.sync.dma_start(out=x_chunk[:], in_=x_by_tile[:, :, j * x_cols : (j + 1) * x_cols])
+                x_raw.append(x_chunk)
+            h_raw = raw.tile([P, M_TILES, H], BF16)
+            nc.sync.dma_start(out=h_raw[:], in_=h.rearrange("(m p) k -> p m k", p=P))
             for quad in range(4):
                 nc.sync.dma_start(
-                    out=planes[32 * quad : 32 * quad + 4, CHUNKS, :].bitcast(I32),
+                    out=planes[32 * quad : 32 * quad + 4, PLANE_TILES, :].bitcast(I32),
                     in_=Whh_scales[0, 4 * quad : 4 * quad + 4, :].bitcast(I32),
                 )
-            for j in range(CHUNKS):
+            for j in range(PLANE_TILES):
                 for quad in range(4):
                     nc.sync.dma_start(
                         out=planes[32 * quad : 32 * quad + 16, j, :].bitcast(I32),
                         in_=Wih_scales[
-                            PASSES_PER_CHUNK * j : PASSES_PER_CHUNK * (j + 1), 4 * quad : 4 * quad + 4, :
+                            PLANES_PER_TILE * j : PLANES_PER_TILE * (j + 1), 4 * quad : 4 * quad + 4, :
                         ].bitcast(I32),
                     )
             whh = keep.tile([P, GATES * H * PACK], U8, align_bytes=64)
             nc.sync.dma_start(out=whh[:].bitcast(I32), in_=Whh_words[0].rearrange("p n t -> p (n t)").bitcast(I32))
+            c_raw = keep.tile([P, M_TILES, H], BF16)
+            nc.sync.dma_start(out=c_raw[:], in_=c.rearrange("(m p) k -> p m k", p=P))
 
             wih_bytes = Wih_words.rearrange("g p n t -> p g (n t)")
-            w_chunks = {}
+            w_loaded = {}
 
             def load_weights(index):
-                gate, j = divmod(index, CHUNKS)
-                chunk = ring.tile([P, PASSES_PER_CHUNK, H * PACK], U8, tag="w", name="w%d" % index, align_bytes=64)
-                nc.sync.dma_start(
-                    out=chunk[:].bitcast(I32),
-                    in_=wih_bytes[
-                        :,
-                        PASSES_PER_CHUNK * j : PASSES_PER_CHUNK * (j + 1),
-                        gate * H * PACK : (gate + 1) * H * PACK,
-                    ].bitcast(I32),
-                )
-                w_chunks[index] = chunk
+                gate, j = divmod(index, W_TILES_PER_GATE)
+                w = ring.tile([P, PLANES_PER_TILE, H * PACK], U8, tag="slot", name="w%d" % index, align_bytes=64)
+                for first in range(0, PLANES_PER_TILE, PASSES_PER_LOAD):
+                    g = PLANES_PER_TILE * j + first
+                    nc.sync.dma_start(
+                        out=w[:, first : first + PASSES_PER_LOAD, :].bitcast(I32),
+                        in_=wih_bytes[:, g : g + PASSES_PER_LOAD, gate * H * PACK : (gate + 1) * H * PACK].bitcast(I32),
+                    )
+                w_loaded[index] = w
 
-            for index in range(RING):
+            for index in range(RING - X_CHUNKS):
                 load_weights(index)
 
             spread = keep.tile([P, ROWS, H], BF16)
             for r in range(0, ROWS, 2):
-                both = psum.tile([P, 2, H], BF16, tag="work")
+                both = banks.tile([P, 2, H], BF16, tag="bank")
                 for i in range(2):
                     nc.tensor.matmul(
                         both[:, i, :],
@@ -212,64 +202,34 @@ def tile_hyperlstmcell_pb_k_kernel(
                     )
                 nc.scalar.copy(out=spread[:, r : r + 2, :], in_=both[:])
 
-            x_codes = keep.tile([P, X_PASSES, BATCH], U32, align_bytes=64)
-            x_scales = keep.tile([P, X_PASSES, BATCH], U8, align_bytes=64)
-            for j in range(CHUNKS):
-                grouped = raw.tile([P, PASSES_PER_CHUNK, BATCH, PACK], BF16, tag="grouped", bufs=2, align_bytes=64)
-                these = slice(PASSES_PER_CHUNK * j, PASSES_PER_CHUNK * (j + 1))
-                transpose_and_quantise(
-                    nc,
-                    psum,
-                    grouped,
-                    [x_raw[j][:, m, :].bitcast(F32) for m in range(M_TILES)],
-                    PASSES_PER_CHUNK,
-                    ident_f32,
-                    x_codes[:, these, :],
-                    x_scales[:, these, :],
-                )
-            h_codes = keep.tile([P, 1, BATCH], U32, align_bytes=64)
-            h_scales = keep.tile([P, 1, BATCH], U8, align_bytes=64)
-            h_grouped = raw.tile([P, 1, BATCH, PACK], BF16, align_bytes=64)
-            transpose_and_quantise(
-                nc,
-                psum,
-                h_grouped,
-                [h_raw[:, m, :].bitcast(F32) for m in range(M_TILES)],
-                1,
-                ident_f32,
-                h_codes[:],
-                h_scales[:],
-            )
-
             emb_t = {}
             ws_t = {}
             for which in ("x", "h", "b"):
-                emb_t[which] = keep.tile([P, GATES, BATCH], BF16, name="emb_t_" + which)
+                emb_t[which] = raw.tile([P, GATES, BATCH], BF16, name="emb_t_" + which)
                 for first in range(0, GATES, 2):
-                    flipped = psum.tile([P, 2, M_TILES, P], BF16, tag="work")
+                    flipped = banks.tile([P, 2, M_TILES, P], BF16, tag="bank")
                     for i in range(2):
-                        for m in range(M_TILES):
+                        for m in batch_tiles:
                             nc.tensor.transpose(
                                 flipped[:, i, m, :],
                                 emb_raw[which][:, m, (first + i) * E : (first + i + 1) * E],
                                 ident_bf16[:],
                             )
-                    nc.scalar.copy(
+                    copy = nc.vector.tensor_copy if first == 0 else nc.scalar.copy
+                    copy(
                         out=emb_t[which][:, first : first + 2, :].rearrange("e g b -> e (g b)"),
                         in_=flipped[:].rearrange("e g m b -> e (g m b)"),
                     )
-                ws_t[which] = keep.tile([P, GATES, H], BF16, name="ws_t_" + which)
+                ws_t[which] = raw.tile([P, GATES, H], BF16, name="ws_t_" + which)
                 for gate in range(GATES):
-                    flipped = psum.tile([P, PACK, P], BF16, tag="work")
+                    flipped = banks.tile([P, PACK, P], BF16, tag="bank")
                     for t in range(PACK):
                         nc.tensor.transpose(flipped[:, t, :], ws_raw[which][:, gate, t, :], ident_bf16[:])
-                    nc.scalar.copy(out=ws_t[which][:, gate, :], in_=flipped[:].rearrange("e t q -> e (t q)"))
-
-        with tc.tile_pool(name="late", bufs=1, reuse_waits="tile") as late, tc.tile_pool(name="work", bufs=2, reuse_waits="tile") as work:
-            tiles = [(gate, m) for gate in range(GATES) for m in range(M_TILES)]
+                    copy = nc.vector.tensor_copy if gate % 2 == 0 else nc.scalar.copy
+                    copy(out=ws_t[which][:, gate, :], in_=flipped[:].rearrange("e t q -> e (t q)"))
 
             def expand(which, gate, m):
-                z = psum.tile([P, H], F32, tag="work")
+                z = banks.tile([P, H], F32, tag="bank")
                 nc.tensor.matmul(
                     z[:],
                     lhsT=emb_t[which][:, gate, m * P : (m + 1) * P],
@@ -279,98 +239,132 @@ def tile_hyperlstmcell_pb_k_kernel(
                 )
                 return z
 
+            assert X_CHUNKS == GATES
+            x_codes = keep.tile([P, X_PASSES, BATCH], U32, align_bytes=64)
+            x_scales = keep.tile([P, X_PASSES, BATCH], U8, align_bytes=64)
             zx = {}
             zh = {}
             rest = {}
-            for gate, m in tiles:
-                zx[gate, m] = late.tile([P, H], F32, name="zx%d_%d" % (gate, m))
-                nc.scalar.copy(out=units_as_pairs(zx[gate, m][:]), in_=units_in_order(expand("x", gate, m)[:]))
-                zh[gate, m] = late.tile([P, H], F32, name="zh%d_%d" % (gate, m))
-                nc.scalar.copy(out=units_as_pairs(zh[gate, m][:]), in_=units_in_order(expand("h", gate, m)[:]))
-                rest[gate, m] = late.tile([P, H], F32, name="rest%d_%d" % (gate, m))
-                nc.vector.tensor_tensor(
-                    out=units_as_pairs(rest[gate, m][:]),
-                    in0=units_in_order(expand("b", gate, m)[:]),
-                    in1=units_as_pairs(spread[:, ROW_BIAS + gate, :]),
-                    op=ALU.add,
-                )
-            for gate, m in tiles:
-                hh = psum.tile([P, H], F32, tag="work")
+            waiting = None
+            for j in range(X_CHUNKS):
+                grouped = raw.tile([P, PASSES_PER_CHUNK, BATCH, PACK], BF16, tag="grouped", bufs=2, align_bytes=64)
+                words = [x_raw[j][:, m, :].bitcast(F32) for m in batch_tiles]
+                for g in range(PASSES_PER_CHUNK):
+                    copy = nc.vector.tensor_copy if g % 2 == 0 else nc.scalar.copy
+                    flip_pass(nc, banks, words, g, ident_f32, grouped[:, g], copy)
+                    if g == 0 and waiting is not None:
+                        quantise(nc, *waiting)
+                these = slice(PASSES_PER_CHUNK * j, PASSES_PER_CHUNK * (j + 1))
+                waiting = (grouped, x_codes[:, these, :], x_scales[:, these, :])
+
+                gate = j
+                for m in batch_tiles:
+                    zx[gate, m] = late.tile([P, H], F32, name="zx%d_%d" % (gate, m))
+                    nc.scalar.copy(out=units_as_pairs(zx[gate, m][:]), in_=units_in_order(expand("x", gate, m)[:]))
+                    zh[gate, m] = late.tile([P, H], F32, name="zh%d_%d" % (gate, m))
+                    nc.scalar.copy(out=units_as_pairs(zh[gate, m][:]), in_=units_in_order(expand("h", gate, m)[:]))
+                    rest[gate, m] = late.tile([P, H], F32, name="rest%d_%d" % (gate, m))
+                    nc.vector.tensor_tensor(
+                        out=units_as_pairs(rest[gate, m][:]),
+                        in0=units_in_order(expand("b", gate, m)[:]),
+                        in1=units_as_pairs(spread[:, ROW_BIAS + gate, :]),
+                        op=ALU.add,
+                    )
+
+            h_codes = keep.tile([P, 1, BATCH], U32, align_bytes=64)
+            h_scales = keep.tile([P, 1, BATCH], U8, align_bytes=64)
+            h_grouped = raw.tile([P, 1, BATCH, PACK], BF16, align_bytes=64)
+            flip_pass(
+                nc, banks, [h_raw[:, m, :].bitcast(F32) for m in batch_tiles], 0, ident_f32, h_grouped[:, 0],
+                nc.vector.tensor_copy,
+            )
+            quantise(nc, *waiting)
+            quantise(nc, h_grouped, h_codes[:], h_scales[:])
+
+        for index in range(RING - X_CHUNKS, RING):
+            load_weights(index)
+
+        for gate in range(GATES):
+            for m in batch_tiles:
+                hh = banks.tile([P, H], F32, tag="bank")
                 nc.tensor.matmul_mx(
                     out=hh[:],
                     lhsT=h_codes[:, 0, m * P : (m + 1) * P].bitcast(FP8X4),
                     lhsT_scale=h_scales[:, 0, m * P : (m + 1) * P],
                     rhs=whh[:, gate * H * PACK : (gate + 1) * H * PACK].bitcast(FP8X4),
-                    rhs_scale=planes[:, CHUNKS, gate * H : (gate + 1) * H],
+                    rhs_scale=planes[:, PLANE_TILES, gate * H : (gate + 1) * H],
                     start=True,
                     stop=True,
                 )
                 nc.vector.tensor_tensor(out=zh[gate, m][:], in0=hh[:], in1=zh[gate, m][:], op=ALU.mult)
-                nc.vector.tensor_tensor(out=rest[gate, m][:], in0=rest[gate, m][:], in1=zh[gate, m][:], op=ALU.add)
+                nc.gpsimd.tensor_tensor(out=rest[gate, m][:], in0=rest[gate, m][:], in1=zh[gate, m][:], op=ALU.add)
 
-            squashed = {}
-            tanh_c = {}
-            for gate in range(GATES):
-                xh = [sums.tile([P, H], F32, tag="xh", name="xh%d_%d" % (gate, m)) for m in range(M_TILES)]
-                for j in range(CHUNKS):
-                    index = gate * CHUNKS + j
-                    for i in range(PASSES_PER_CHUNK):
-                        g = PASSES_PER_CHUNK * j + i
-                        for m in range(M_TILES):
+        work = ctx.enter_context(tc.tile_pool(name="work", bufs=2, reuse_waits="tile"))
+        acts = ctx.enter_context(tc.tile_pool(name="acts", bufs=1, reuse_waits="tile"))
+        squashed = {}
+        for gate in range(GATES):
+            xh = [banks.tile([P, H], F32, tag="bank", name="xh%d_%d" % (gate, m)) for m in batch_tiles]
+            for j in range(W_TILES_PER_GATE):
+                index = gate * W_TILES_PER_GATE + j
+                for first in range(0, PLANES_PER_TILE, PASSES_PER_LOAD):
+                    for m in batch_tiles:
+                        for i in range(first, first + PASSES_PER_LOAD):
+                            g = PLANES_PER_TILE * j + i
                             nc.tensor.matmul_mx(
                                 out=xh[m][:],
                                 lhsT=x_codes[:, g, m * P : (m + 1) * P].bitcast(FP8X4),
                                 lhsT_scale=x_scales[:, g, m * P : (m + 1) * P],
-                                rhs=w_chunks[index][:, i, :].bitcast(FP8X4),
+                                rhs=w_loaded[index][:, i, :].bitcast(FP8X4),
                                 rhs_scale=planes[4 * i : P, j, gate * H : (gate + 1) * H],
                                 start=(g == 0),
                                 stop=(g == X_PASSES - 1),
                             )
-                    if index + RING < GATES * CHUNKS:
-                        load_weights(index + RING)
+                if index + RING < GATES * W_TILES_PER_GATE:
+                    load_weights(index + RING)
 
-                for m in range(M_TILES):
-                    pre = work.tile([P, H], F32, tag="pre")
-                    nc.vector.tensor_tensor(out=pre[:], in0=xh[m][:], in1=zx[gate, m][:], op=ALU.mult)
+            halfway = []
+            for m in batch_tiles:
+                pre = work.tile([P, H], F32, tag="pre")
+                nc.vector.tensor_tensor(out=pre[:], in0=xh[m][:], in1=zx[gate, m][:], op=ALU.mult)
+                total = stat.tile([P, 1], F32, tag="total")
+                nc.vector.scalar_tensor_tensor(
+                    out=pre[:], in0=pre[:], scalar=1.0, in1=rest[gate, m][:], op0=ALU.mult, op1=ALU.add,
+                    accum_out=total[:],
+                )
+                halfway.append(norm_first_half(nc, work, stat, half, pre[:], total, spread[:, ROW_GAMMA + gate, :]))
+            for m in batch_tiles:
+                centred, root = halfway[m]
+                norm_second_half(nc, stat, centred, root, spread[:, ROW_BETA + gate, :], centred[:])
+                squashed[gate, m] = acts.tile([P, H], F32, name="squashed%d_%d" % (gate, m))
+                nc.scalar.activation(
+                    out=squashed[gate, m][:], in_=centred[:], func=(ACT.Tanh if gate == GATE_G else ACT.Sigmoid)
+                )
+
+            if gate == GATE_F:
+                for m in batch_tiles:
+                    nc.vector.tensor_tensor(
+                        out=squashed[GATE_F, m][:], in0=squashed[GATE_F, m][:], in1=c_raw[:, m, :], op=ALU.mult
+                    )
+            if gate == GATE_G:
+                halfway = []
+                for m in batch_tiles:
+                    cell = squashed[GATE_I, m]
+                    nc.vector.tensor_tensor(out=cell[:], in0=cell[:], in1=squashed[GATE_G, m][:], op=ALU.mult)
                     total = stat.tile([P, 1], F32, tag="total")
                     nc.vector.scalar_tensor_tensor(
-                        out=pre[:], in0=pre[:], scalar=1.0, in1=rest[gate, m][:], op0=ALU.mult, op1=ALU.add,
+                        out=cell[:], in0=cell[:], scalar=1.0, in1=squashed[GATE_F, m][:], op0=ALU.mult, op1=ALU.add,
                         accum_out=total[:],
                     )
-                    normed = work.tile([P, H], F32, tag="normed")
-                    layer_norm(
-                        nc, work, stat, half, pre[:], total,
-                        spread[:, ROW_GAMMA + gate, :], spread[:, ROW_BETA + gate, :], normed[:],
-                    )
-                    squashed[gate, m] = late.tile([P, H], F32, name="squashed%d_%d" % (gate, m))
-                    nc.scalar.activation(
-                        out=squashed[gate, m][:], in_=normed[:], func=(ACT.Tanh if gate == GATE_G else ACT.Sigmoid)
-                    )
-
-                if gate == GATE_F:
-                    for m in range(M_TILES):
-                        nc.vector.tensor_tensor(
-                            out=squashed[GATE_F, m][:], in0=squashed[GATE_F, m][:], in1=c_raw[:, m, :], op=ALU.mult
-                        )
-                if gate == GATE_G:
-                    for m in range(M_TILES):
-                        nc.vector.tensor_tensor(
-                            out=squashed[GATE_I, m][:], in0=squashed[GATE_I, m][:], in1=squashed[GATE_G, m][:], op=ALU.mult
-                        )
-                        total = stat.tile([P, 1], F32, tag="total")
-                        nc.vector.scalar_tensor_tensor(
-                            out=squashed[GATE_I, m][:], in0=squashed[GATE_I, m][:], scalar=1.0, in1=squashed[GATE_F, m][:],
-                            op0=ALU.mult, op1=ALU.add, accum_out=total[:],
-                        )
-                        new_c = late.tile([P, H], F32, name="new_c%d" % m)
-                        layer_norm(
-                            nc, work, stat, half, squashed[GATE_I, m][:], total,
-                            spread[:, ROW_CELL_GAMMA, :], spread[:, ROW_CELL_BETA, :], new_c[:],
-                        )
-                        nc.sync.dma_start(out=out_1[m * P : (m + 1) * P, :], in_=new_c[:])
-                        tanh_c[m] = late.tile([P, H], F32, name="tanh_c%d" % m)
-                        nc.scalar.activation(out=tanh_c[m][:], in_=new_c[:], func=ACT.Tanh)
-                if gate == GATE_O:
-                    for m in range(M_TILES):
-                        nc.vector.tensor_tensor(out=tanh_c[m][:], in0=tanh_c[m][:], in1=squashed[GATE_O, m][:], op=ALU.mult)
-                        nc.sync.dma_start(out=out_0[m * P : (m + 1) * P, :], in_=tanh_c[m][:])
+                    halfway.append(norm_first_half(nc, work, stat, half, cell[:], total, spread[:, ROW_CELL_GAMMA, :]))
+                tanh_c = []
+                for m in batch_tiles:
+                    centred, root = halfway[m]
+                    new_c = acts.tile([P, H], F32, name="new_c%d" % m)
+                    norm_second_half(nc, stat, centred, root, spread[:, ROW_CELL_BETA, :], new_c[:])
+                    nc.sync.dma_start(out=out_1[m * P : (m + 1) * P, :], in_=new_c[:])
+                    tanh_c.append(acts.tile([P, H], F32, name="tanh_c%d" % m))
+                    nc.scalar.activation(out=tanh_c[m][:], in_=new_c[:], func=ACT.Tanh)
+            if gate == GATE_O:
+                for m in batch_tiles:
+                    nc.vector.tensor_tensor(out=tanh_c[m][:], in0=tanh_c[m][:], in1=squashed[GATE_O, m][:], op=ALU.mult)
+                    nc.sync.dma_start(out=out_0[m * P : (m + 1) * P, :], in_=tanh_c[m][:])

@@ -32,7 +32,6 @@ EPS = 1e-6
 FLOPS = 2 * BATCH * (IN + H) * GATES * H + 3 * 2 * BATCH * GATES * H * E
 
 ROW_GAMMA, ROW_BETA, ROW_BIAS, ROW_CELL_GAMMA, ROW_CELL_BETA = 0, 4, 8, 12, 13
-ROWS = 14
 
 
 def units_in_order(ap):
@@ -52,6 +51,15 @@ def flip_pass(nc, banks, words, g, ident_f32, grouped, engine_copy):
     engine_copy(out=side_by_side, in_=flipped[:].rearrange("p m u b -> p m b u"))
 
 
+def spread_rows(nc, banks, ident_bf16, rows, chosen):
+    both = banks.tile([P, 2, H], BF16, tag="bank")
+    for i, r in enumerate(chosen):
+        nc.tensor.matmul(
+            both[:, i, :], lhsT=ident_bf16[:, r : r + 1].to_broadcast([P, P]), rhs=rows[:], start=True, stop=True
+        )
+    return both
+
+
 def quantise(nc, grouped, codes, scales):
     nc.vector.quantize_mx(
         out=codes.rearrange("p g c -> p (g c)").bitcast(FP8X4),
@@ -60,9 +68,7 @@ def quantise(nc, grouped, codes, scales):
     )
 
 
-def norm_first_half(nc, work, stat, half, values, total, gamma):
-    minus_mean = stat.tile([P, 1], F32, tag="minus_mean")
-    nc.vector.tensor_scalar(out=minus_mean[:], in0=total[:], scalar1=-1.0 / H, scalar2=None, op0=ALU.mult)
+def norm_first_half(nc, work, stat, half, values, minus_mean, gamma):
     squares = work.tile([P, H], F32, tag="squares")
     sum_of_squares = stat.tile([P, 1], F32, tag="sum_of_squares")
     nc.scalar.activation(out=squares[:], in_=values, func=ACT.Square, bias=minus_mean[:], accum_out=sum_of_squares[:])
@@ -73,13 +79,15 @@ def norm_first_half(nc, work, stat, half, values, total, gamma):
     return centred, root
 
 
-def norm_second_half(nc, stat, centred, root, beta, out):
-    inverse = stat.tile([P, 1], F32, tag="inverse")
+def norm_second_half(nc, stat, centred, root, beta):
+    divisor = stat.tile([P, 1], F32, tag="divisor")
     nc.vector.tensor_scalar(
-        out=inverse[:], in0=root[:], scalar1=1.0 / math.sqrt(H - 1), scalar2=EPS, op0=ALU.mult, op1=ALU.add
+        out=divisor[:], in0=root[:], scalar1=1.0 / math.sqrt(H - 1), scalar2=EPS, op0=ALU.mult, op1=ALU.add
     )
-    nc.vector.reciprocal(out=inverse[:], in_=inverse[:])
-    nc.vector.scalar_tensor_tensor(out=out, in0=centred[:], scalar=inverse[:], in1=beta, op0=ALU.mult, op1=ALU.add)
+    nc.vector.scalar_tensor_tensor(out=centred[:], in0=beta, scalar=divisor[:], in1=centred[:], op0=ALU.mult, op1=ALU.add)
+    inverse = stat.tile([P, 1], F32, tag="inverse")
+    nc.vector.reciprocal(out=inverse[:], in_=divisor[:])
+    return inverse
 
 
 def tile_hyperlstmcell_pb_k_kernel(
@@ -108,201 +116,200 @@ def tile_hyperlstmcell_pb_k_kernel(
     nc = tc.nc
     batch_tiles = range(M_TILES)
     with ExitStack() as ctx:
-        ctx.enter_context(tc.manual_schedule())
         keep = ctx.enter_context(tc.tile_pool(name="keep", bufs=1))
         ring = ctx.enter_context(tc.tile_pool(name="ring", bufs=RING))
         stat = ctx.enter_context(tc.tile_pool(name="stat", bufs=4))
         late = ctx.enter_context(tc.tile_pool(name="late", bufs=1))
         banks = ctx.enter_context(tc.psum_pool(name="banks", bufs=8))
 
-        rows = keep.tile([P, H], BF16)
-        nc.vector.memset(rows[:].bitcast(I32), 0)
-        half = keep.tile([P, 1], F32)
-        nc.vector.memset(half[:], 0.5)
-        ident_bf16 = keep.tile([P, P], BF16)
-        make_identity(nc, ident_bf16[:])
-        ident_f32 = keep.tile([P, P], F32)
-        make_identity(nc, ident_f32[:])
-        warm = keep.tile([P, 1], F32)
-        nc.scalar.activation(out=warm[:], in_=half[:], func=ACT.Sigmoid)
+        with tc.manual_schedule():
+            rows = keep.tile([P, H], BF16)
+            nc.vector.memset(rows[:].bitcast(I32), 0)
+            half = keep.tile([P, 1], F32)
+            nc.vector.memset(half[:], 0.5)
+            ident_bf16 = keep.tile([P, P], BF16)
+            make_identity(nc, ident_bf16[:])
+            ident_f32 = keep.tile([P, P], F32)
+            make_identity(nc, ident_f32[:])
+            warm = keep.tile([P, 1], F32)
+            nc.scalar.activation(out=warm[:], in_=half[:], func=ACT.Sigmoid)
 
-        planes = keep.tile([P, PLANE_TILES + 1, GATES * H], U8, align_bytes=64)
-        nc.vector.memset(planes[:].rearrange("p j n -> p (j n)").bitcast(I32), 0)
+            planes = keep.tile([P, PLANE_TILES + 1, GATES * H], U8, align_bytes=64)
+            nc.vector.memset(planes[:].rearrange("p j n -> p (j n)").bitcast(I32), 0)
 
-        with tc.tile_pool(name="raw", bufs=1) as raw:
-            nc.sync.dma_start(out=rows[ROW_GAMMA : ROW_GAMMA + GATES, :], in_=ln_gamma)
-            nc.sync.dma_start(out=rows[ROW_BETA : ROW_BETA + GATES, :], in_=ln_beta)
-            nc.sync.dma_start(out=rows[ROW_BIAS : ROW_BIAS + GATES, :], in_=bias.rearrange("(g n) -> g n", g=GATES))
-            nc.sync.dma_start(out=rows[ROW_CELL_GAMMA : ROW_CELL_GAMMA + 1, :], in_=lnc_gamma.rearrange("(o n) -> o n", o=1))
-            nc.sync.dma_start(out=rows[ROW_CELL_BETA : ROW_CELL_BETA + 1, :], in_=lnc_beta.rearrange("(o n) -> o n", o=1))
-            emb_raw = {}
-            ws_raw = {}
-            for which, emb, ws in (("x", emb_x, Wsx), ("h", emb_h, Wsh), ("b", emb_b, Wsb)):
-                emb_raw[which] = raw.tile([P, M_TILES, GATES * E], BF16, name="emb_raw_" + which)
-                nc.sync.dma_start(out=emb_raw[which][:], in_=emb.rearrange("(m p) g e -> p m (g e)", p=P))
-                ws_raw[which] = raw.tile([P, GATES, PACK, E], BF16, name="ws_raw_" + which)
-                nc.sync.dma_start(
-                    out=ws_raw[which][:].rearrange("q g t e -> q g (t e)"),
-                    in_=ws.rearrange("g (q t) e -> q g (t e)", t=PACK),
-                )
-            x_by_tile = x.rearrange("(m p) k -> p m k", p=P)
-            x_cols = PASSES_PER_CHUNK * K_PASS
-            x_raw = []
-            for j in range(X_CHUNKS):
-                x_chunk = ring.tile([P, M_TILES, x_cols], BF16, tag="slot", name="x_raw%d" % j, align_bytes=64)
-                nc.sync.dma_start(out=x_chunk[:], in_=x_by_tile[:, :, j * x_cols : (j + 1) * x_cols])
-                x_raw.append(x_chunk)
-            h_raw = raw.tile([P, M_TILES, H], BF16)
-            nc.sync.dma_start(out=h_raw[:], in_=h.rearrange("(m p) k -> p m k", p=P))
-            for quad in range(4):
-                nc.sync.dma_start(
-                    out=planes[32 * quad : 32 * quad + 4, PLANE_TILES, :].bitcast(I32),
-                    in_=Whh_scales[0, 4 * quad : 4 * quad + 4, :].bitcast(I32),
-                )
-            for j in range(PLANE_TILES):
+            with tc.tile_pool(name="raw", bufs=1) as raw:
+                nc.sync.dma_start(out=rows[ROW_GAMMA : ROW_GAMMA + GATES, :], in_=ln_gamma)
+                nc.sync.dma_start(out=rows[ROW_BETA : ROW_BETA + GATES, :], in_=ln_beta)
+                nc.sync.dma_start(out=rows[ROW_BIAS : ROW_BIAS + GATES, :], in_=bias.rearrange("(g n) -> g n", g=GATES))
+                nc.sync.dma_start(out=rows[ROW_CELL_GAMMA : ROW_CELL_GAMMA + 1, :], in_=lnc_gamma.rearrange("(o n) -> o n", o=1))
+                nc.sync.dma_start(out=rows[ROW_CELL_BETA : ROW_CELL_BETA + 1, :], in_=lnc_beta.rearrange("(o n) -> o n", o=1))
+                emb_raw = {}
+                ws_raw = {}
+                for which, emb, ws in (("x", emb_x, Wsx), ("h", emb_h, Wsh), ("b", emb_b, Wsb)):
+                    emb_raw[which] = raw.tile([P, M_TILES, GATES * E], BF16, name="emb_raw_" + which)
+                    nc.sync.dma_start(out=emb_raw[which][:], in_=emb.rearrange("(m p) g e -> p m (g e)", p=P))
+                    ws_raw[which] = raw.tile([P, GATES, PACK, E], BF16, name="ws_raw_" + which)
+                    nc.sync.dma_start(
+                        out=ws_raw[which][:].rearrange("q g t e -> q g (t e)"),
+                        in_=ws.rearrange("g (q t) e -> q g (t e)", t=PACK),
+                    )
+                h_raw = raw.tile([P, M_TILES, H], BF16)
+                nc.sync.dma_start(out=h_raw[:], in_=h.rearrange("(m p) k -> p m k", p=P))
+                x_by_tile = x.rearrange("(m p) k -> p m k", p=P)
+                x_cols = PASSES_PER_CHUNK * K_PASS
+                x_raw = []
+                for j in range(X_CHUNKS):
+                    x_chunk = ring.tile([P, M_TILES, x_cols], BF16, tag="slot", name="x_raw%d" % j, align_bytes=64)
+                    nc.sync.dma_start(out=x_chunk[:], in_=x_by_tile[:, :, j * x_cols : (j + 1) * x_cols])
+                    x_raw.append(x_chunk)
                 for quad in range(4):
                     nc.sync.dma_start(
-                        out=planes[32 * quad : 32 * quad + 16, j, :].bitcast(I32),
-                        in_=Wih_scales[
-                            PLANES_PER_TILE * j : PLANES_PER_TILE * (j + 1), 4 * quad : 4 * quad + 4, :
-                        ].bitcast(I32),
+                        out=planes[32 * quad : 32 * quad + 4, PLANE_TILES, :].bitcast(I32),
+                        in_=Whh_scales[0, 4 * quad : 4 * quad + 4, :].bitcast(I32),
                     )
-            whh = keep.tile([P, GATES * H * PACK], U8, align_bytes=64)
-            nc.sync.dma_start(out=whh[:].bitcast(I32), in_=Whh_words[0].rearrange("p n t -> p (n t)").bitcast(I32))
-            c_raw = keep.tile([P, M_TILES, H], BF16)
-            nc.sync.dma_start(out=c_raw[:], in_=c.rearrange("(m p) k -> p m k", p=P))
+                for j in range(PLANE_TILES):
+                    for quad in range(4):
+                        nc.sync.dma_start(
+                            out=planes[32 * quad : 32 * quad + 16, j, :].bitcast(I32),
+                            in_=Wih_scales[
+                                PLANES_PER_TILE * j : PLANES_PER_TILE * (j + 1), 4 * quad : 4 * quad + 4, :
+                            ].bitcast(I32),
+                        )
+                whh = keep.tile([P, GATES * H * PACK], U8, align_bytes=64)
+                nc.sync.dma_start(out=whh[:].bitcast(I32), in_=Whh_words[0].rearrange("p n t -> p (n t)").bitcast(I32))
+                c_raw = keep.tile([P, M_TILES, H], BF16)
+                nc.sync.dma_start(out=c_raw[:], in_=c.rearrange("(m p) k -> p m k", p=P))
 
-            wih_bytes = Wih_words.rearrange("g p n t -> p g (n t)")
-            w_loaded = {}
+                wih_bytes = Wih_words.rearrange("g p n t -> p g (n t)")
+                w_loaded = {}
 
-            def load_weights(index):
-                gate, j = divmod(index, W_TILES_PER_GATE)
-                w = ring.tile([P, PLANES_PER_TILE, H * PACK], U8, tag="slot", name="w%d" % index, align_bytes=64)
-                for first in range(0, PLANES_PER_TILE, PASSES_PER_LOAD):
-                    g = PLANES_PER_TILE * j + first
-                    nc.sync.dma_start(
-                        out=w[:, first : first + PASSES_PER_LOAD, :].bitcast(I32),
-                        in_=wih_bytes[:, g : g + PASSES_PER_LOAD, gate * H * PACK : (gate + 1) * H * PACK].bitcast(I32),
-                    )
-                w_loaded[index] = w
+                def load_weights(index):
+                    gate, j = divmod(index, W_TILES_PER_GATE)
+                    w = ring.tile([P, PLANES_PER_TILE, H * PACK], U8, tag="slot", name="w%d" % index, align_bytes=64)
+                    for first in range(0, PLANES_PER_TILE, PASSES_PER_LOAD):
+                        g = PLANES_PER_TILE * j + first
+                        nc.sync.dma_start(
+                            out=w[:, first : first + PASSES_PER_LOAD, :].bitcast(I32),
+                            in_=wih_bytes[:, g : g + PASSES_PER_LOAD, gate * H * PACK : (gate + 1) * H * PACK].bitcast(I32),
+                        )
+                    w_loaded[index] = w
 
-            for index in range(RING - X_CHUNKS):
-                load_weights(index)
+                for index in range(RING - X_CHUNKS):
+                    load_weights(index)
 
-            spread = keep.tile([P, ROWS, H], BF16)
-            for r in range(0, ROWS, 2):
-                both = banks.tile([P, 2, H], BF16, tag="bank")
-                for i in range(2):
+                bias_all = keep.tile([P, GATES, H], BF16)
+                for gate in range(0, GATES, 2):
+                    both = spread_rows(nc, banks, ident_bf16, rows, (ROW_BIAS + gate, ROW_BIAS + gate + 1))
+                    nc.scalar.copy(out=bias_all[:, gate : gate + 2, :], in_=both[:])
+
+                emb_t = {}
+                ws_t = {}
+                for which in ("x", "h", "b"):
+                    emb_t[which] = raw.tile([P, GATES, BATCH], BF16, name="emb_t_" + which)
+                    for first in range(0, GATES, 2):
+                        flipped = banks.tile([P, 2, M_TILES, P], BF16, tag="bank")
+                        for i in range(2):
+                            for m in batch_tiles:
+                                nc.tensor.transpose(
+                                    flipped[:, i, m, :],
+                                    emb_raw[which][:, m, (first + i) * E : (first + i + 1) * E],
+                                    ident_bf16[:],
+                                )
+                        copy = nc.vector.tensor_copy if first == 0 else nc.scalar.copy
+                        copy(
+                            out=emb_t[which][:, first : first + 2, :].rearrange("e g b -> e (g b)"),
+                            in_=flipped[:].rearrange("e g m b -> e (g m b)"),
+                        )
+                    ws_t[which] = raw.tile([P, GATES, H], BF16, name="ws_t_" + which)
+                    for gate in range(GATES):
+                        flipped = banks.tile([P, PACK, P], BF16, tag="bank")
+                        for t in range(PACK):
+                            nc.tensor.transpose(flipped[:, t, :], ws_raw[which][:, gate, t, :], ident_bf16[:])
+                        copy = nc.vector.tensor_copy if gate % 2 == 0 else nc.scalar.copy
+                        copy(out=ws_t[which][:, gate, :], in_=flipped[:].rearrange("e t q -> e (t q)"))
+
+                def expand(which, gate, m):
+                    z = banks.tile([P, H], F32, tag="bank")
                     nc.tensor.matmul(
-                        both[:, i, :],
-                        lhsT=ident_bf16[:, r + i : r + i + 1].to_broadcast([P, P]),
-                        rhs=rows[:],
+                        z[:],
+                        lhsT=emb_t[which][:, gate, m * P : (m + 1) * P],
+                        rhs=ws_t[which][:, gate, :],
                         start=True,
                         stop=True,
                     )
-                nc.scalar.copy(out=spread[:, r : r + 2, :], in_=both[:])
+                    return z
 
-            emb_t = {}
-            ws_t = {}
-            for which in ("x", "h", "b"):
-                emb_t[which] = raw.tile([P, GATES, BATCH], BF16, name="emb_t_" + which)
-                for first in range(0, GATES, 2):
-                    flipped = banks.tile([P, 2, M_TILES, P], BF16, tag="bank")
-                    for i in range(2):
-                        for m in batch_tiles:
-                            nc.tensor.transpose(
-                                flipped[:, i, m, :],
-                                emb_raw[which][:, m, (first + i) * E : (first + i + 1) * E],
-                                ident_bf16[:],
-                            )
-                    copy = nc.vector.tensor_copy if first == 0 else nc.scalar.copy
-                    copy(
-                        out=emb_t[which][:, first : first + 2, :].rearrange("e g b -> e (g b)"),
-                        in_=flipped[:].rearrange("e g m b -> e (g m b)"),
-                    )
-                ws_t[which] = raw.tile([P, GATES, H], BF16, name="ws_t_" + which)
-                for gate in range(GATES):
-                    flipped = banks.tile([P, PACK, P], BF16, tag="bank")
-                    for t in range(PACK):
-                        nc.tensor.transpose(flipped[:, t, :], ws_raw[which][:, gate, t, :], ident_bf16[:])
-                    copy = nc.vector.tensor_copy if gate % 2 == 0 else nc.scalar.copy
-                    copy(out=ws_t[which][:, gate, :], in_=flipped[:].rearrange("e t q -> e (t q)"))
-
-            def expand(which, gate, m):
-                z = banks.tile([P, H], F32, tag="bank")
-                nc.tensor.matmul(
-                    z[:],
-                    lhsT=emb_t[which][:, gate, m * P : (m + 1) * P],
-                    rhs=ws_t[which][:, gate, :],
-                    start=True,
-                    stop=True,
+                h_codes = keep.tile([P, 1, BATCH], U32, align_bytes=64)
+                h_scales = keep.tile([P, 1, BATCH], U8, align_bytes=64)
+                h_grouped = raw.tile([P, 1, BATCH, PACK], BF16, align_bytes=64)
+                flip_pass(
+                    nc, banks, [h_raw[:, m, :].bitcast(F32) for m in batch_tiles], 0, ident_f32, h_grouped[:, 0],
+                    nc.vector.tensor_copy,
                 )
-                return z
 
-            assert X_CHUNKS == GATES
-            x_codes = keep.tile([P, X_PASSES, BATCH], U32, align_bytes=64)
-            x_scales = keep.tile([P, X_PASSES, BATCH], U8, align_bytes=64)
-            zx = {}
-            zh = {}
-            rest = {}
-            waiting = None
-            for j in range(X_CHUNKS):
-                grouped = raw.tile([P, PASSES_PER_CHUNK, BATCH, PACK], BF16, tag="grouped", bufs=2, align_bytes=64)
-                words = [x_raw[j][:, m, :].bitcast(F32) for m in batch_tiles]
-                for g in range(PASSES_PER_CHUNK):
-                    copy = nc.vector.tensor_copy if g % 2 == 0 else nc.scalar.copy
-                    flip_pass(nc, banks, words, g, ident_f32, grouped[:, g], copy)
-                    if g == 0 and waiting is not None:
-                        quantise(nc, *waiting)
-                these = slice(PASSES_PER_CHUNK * j, PASSES_PER_CHUNK * (j + 1))
-                waiting = (grouped, x_codes[:, these, :], x_scales[:, these, :])
+                assert X_CHUNKS == GATES
+                x_codes = keep.tile([P, X_PASSES, BATCH], U32, align_bytes=64)
+                x_scales = keep.tile([P, X_PASSES, BATCH], U8, align_bytes=64)
+                zx = {}
+                zh = {}
+                rest = {}
+                waiting = (h_grouped, h_codes[:], h_scales[:])
+                for j in range(X_CHUNKS):
+                    grouped = raw.tile([P, PASSES_PER_CHUNK, BATCH, PACK], BF16, tag="grouped", bufs=2, align_bytes=64)
+                    words = [x_raw[j][:, m, :].bitcast(F32) for m in batch_tiles]
+                    for g in range(PASSES_PER_CHUNK):
+                        copy = nc.vector.tensor_copy if g % 2 == 0 else nc.scalar.copy
+                        flip_pass(nc, banks, words, g, ident_f32, grouped[:, g], copy)
+                        if g == 0:
+                            quantise(nc, *waiting)
+                    these = slice(PASSES_PER_CHUNK * j, PASSES_PER_CHUNK * (j + 1))
+                    waiting = (grouped, x_codes[:, these, :], x_scales[:, these, :])
 
-                gate = j
+                    gate = j
+                    for m in batch_tiles:
+                        zx[gate, m] = late.tile([P, H], F32, name="zx%d_%d" % (gate, m))
+                        nc.scalar.copy(out=units_as_pairs(zx[gate, m][:]), in_=units_in_order(expand("x", gate, m)[:]))
+                        zh[gate, m] = late.tile([P, H], F32, name="zh%d_%d" % (gate, m))
+                        nc.scalar.copy(out=units_as_pairs(zh[gate, m][:]), in_=units_in_order(expand("h", gate, m)[:]))
+                        rest[gate, m] = late.tile([P, H], F32, name="rest%d_%d" % (gate, m))
+                        nc.vector.tensor_tensor(
+                            out=units_as_pairs(rest[gate, m][:]),
+                            in0=units_in_order(expand("b", gate, m)[:]),
+                            in1=units_as_pairs(bias_all[:, gate, :]),
+                            op=ALU.add,
+                        )
+
+                quantise(nc, *waiting)
+
+            for index in range(RING - X_CHUNKS, RING):
+                load_weights(index)
+
+            work = ctx.enter_context(tc.tile_pool(name="work", bufs=4, reuse_waits="tile"))
+            acts = ctx.enter_context(tc.tile_pool(name="acts", bufs=1, reuse_waits="tile"))
+            rest_sum = {}
+            for gate in range(GATES):
                 for m in batch_tiles:
-                    zx[gate, m] = late.tile([P, H], F32, name="zx%d_%d" % (gate, m))
-                    nc.scalar.copy(out=units_as_pairs(zx[gate, m][:]), in_=units_in_order(expand("x", gate, m)[:]))
-                    zh[gate, m] = late.tile([P, H], F32, name="zh%d_%d" % (gate, m))
-                    nc.scalar.copy(out=units_as_pairs(zh[gate, m][:]), in_=units_in_order(expand("h", gate, m)[:]))
-                    rest[gate, m] = late.tile([P, H], F32, name="rest%d_%d" % (gate, m))
-                    nc.vector.tensor_tensor(
-                        out=units_as_pairs(rest[gate, m][:]),
-                        in0=units_in_order(expand("b", gate, m)[:]),
-                        in1=units_as_pairs(spread[:, ROW_BIAS + gate, :]),
-                        op=ALU.add,
+                    hh = banks.tile([P, H], F32, tag="bank")
+                    nc.tensor.matmul_mx(
+                        out=hh[:],
+                        lhsT=h_codes[:, 0, m * P : (m + 1) * P].bitcast(FP8X4),
+                        lhsT_scale=h_scales[:, 0, m * P : (m + 1) * P],
+                        rhs=whh[:, gate * H * PACK : (gate + 1) * H * PACK].bitcast(FP8X4),
+                        rhs_scale=planes[:, PLANE_TILES, gate * H : (gate + 1) * H],
+                        start=True,
+                        stop=True,
                     )
+                    nc.vector.tensor_tensor(out=zh[gate, m][:], in0=hh[:], in1=zh[gate, m][:], op=ALU.mult)
+                    nc.gpsimd.tensor_tensor(out=rest[gate, m][:], in0=rest[gate, m][:], in1=zh[gate, m][:], op=ALU.add)
+                    unused = work.tile([P, H], F32, tag="squares")
+                    rest_sum[gate, m] = keep.tile([P, 1], F32, name="rest_sum%d_%d" % (gate, m))
+                    nc.scalar.activation(out=unused[:], in_=rest[gate, m][:], func=ACT.Copy, accum_out=rest_sum[gate, m][:])
 
-            h_codes = keep.tile([P, 1, BATCH], U32, align_bytes=64)
-            h_scales = keep.tile([P, 1, BATCH], U8, align_bytes=64)
-            h_grouped = raw.tile([P, 1, BATCH, PACK], BF16, align_bytes=64)
-            flip_pass(
-                nc, banks, [h_raw[:, m, :].bitcast(F32) for m in batch_tiles], 0, ident_f32, h_grouped[:, 0],
-                nc.vector.tensor_copy,
-            )
-            quantise(nc, *waiting)
-            quantise(nc, h_grouped, h_codes[:], h_scales[:])
-
-        for index in range(RING - X_CHUNKS, RING):
-            load_weights(index)
-
-        for gate in range(GATES):
-            for m in batch_tiles:
-                hh = banks.tile([P, H], F32, tag="bank")
-                nc.tensor.matmul_mx(
-                    out=hh[:],
-                    lhsT=h_codes[:, 0, m * P : (m + 1) * P].bitcast(FP8X4),
-                    lhsT_scale=h_scales[:, 0, m * P : (m + 1) * P],
-                    rhs=whh[:, gate * H * PACK : (gate + 1) * H * PACK].bitcast(FP8X4),
-                    rhs_scale=planes[:, PLANE_TILES, gate * H : (gate + 1) * H],
-                    start=True,
-                    stop=True,
-                )
-                nc.vector.tensor_tensor(out=zh[gate, m][:], in0=hh[:], in1=zh[gate, m][:], op=ALU.mult)
-                nc.gpsimd.tensor_tensor(out=rest[gate, m][:], in0=rest[gate, m][:], in1=zh[gate, m][:], op=ALU.add)
-
-        work = ctx.enter_context(tc.tile_pool(name="work", bufs=2, reuse_waits="tile"))
-        acts = ctx.enter_context(tc.tile_pool(name="acts", bufs=1, reuse_waits="tile"))
         squashed = {}
         for gate in range(GATES):
+            gamma_beta = spread_rows(nc, banks, ident_bf16, rows, (ROW_GAMMA + gate, ROW_BETA + gate))
+            if gate == GATE_O:
+                cell_gamma_beta = spread_rows(nc, banks, ident_bf16, rows, (ROW_CELL_GAMMA, ROW_CELL_BETA))
             xh = [banks.tile([P, H], F32, tag="bank", name="xh%d_%d" % (gate, m)) for m in batch_tiles]
             for j in range(W_TILES_PER_GATE):
                 index = gate * W_TILES_PER_GATE + j
@@ -322,49 +329,55 @@ def tile_hyperlstmcell_pb_k_kernel(
                 if index + RING < GATES * W_TILES_PER_GATE:
                     load_weights(index + RING)
 
-            halfway = []
+            pre = [work.tile([P, H], F32, tag="pre", name="pre%d" % m) for m in batch_tiles]
+            minus_mean = [stat.tile([P, 1], F32, tag="minus_mean", name="minus_mean%d" % m) for m in batch_tiles]
             for m in batch_tiles:
-                pre = work.tile([P, H], F32, tag="pre")
-                nc.vector.tensor_tensor(out=pre[:], in0=xh[m][:], in1=zx[gate, m][:], op=ALU.mult)
-                total = stat.tile([P, 1], F32, tag="total")
+                product_sum = stat.tile([P, 1], F32, tag="product_sum")
                 nc.vector.scalar_tensor_tensor(
-                    out=pre[:], in0=pre[:], scalar=1.0, in1=rest[gate, m][:], op0=ALU.mult, op1=ALU.add,
-                    accum_out=total[:],
+                    out=pre[m][:], in0=xh[m][:], scalar=1.0, in1=zx[gate, m][:], op0=ALU.mult, op1=ALU.mult,
+                    accum_out=product_sum[:],
                 )
-                halfway.append(norm_first_half(nc, work, stat, half, pre[:], total, spread[:, ROW_GAMMA + gate, :]))
+                nc.vector.tensor_scalar(
+                    out=minus_mean[m][:], in0=product_sum[:], scalar1=rest_sum[gate, m][:], scalar2=-1.0 / H,
+                    op0=ALU.add, op1=ALU.mult,
+                )
+            for m in batch_tiles:
+                nc.vector.tensor_tensor(out=pre[m][:], in0=pre[m][:], in1=rest[gate, m][:], op=ALU.add)
+            halfway = [
+                norm_first_half(nc, work, stat, half, pre[m][:], minus_mean[m], gamma_beta[:, 0, :]) for m in batch_tiles
+            ]
             for m in batch_tiles:
                 centred, root = halfway[m]
-                norm_second_half(nc, stat, centred, root, spread[:, ROW_BETA + gate, :], centred[:])
+                inverse = norm_second_half(nc, stat, centred, root, gamma_beta[:, 1, :])
                 squashed[gate, m] = acts.tile([P, H], F32, name="squashed%d_%d" % (gate, m))
                 nc.scalar.activation(
-                    out=squashed[gate, m][:], in_=centred[:], func=(ACT.Tanh if gate == GATE_G else ACT.Sigmoid)
+                    out=squashed[gate, m][:], in_=centred[:], func=(ACT.Tanh if gate == GATE_G else ACT.Sigmoid),
+                    scale=inverse[:],
                 )
 
-            if gate == GATE_F:
-                for m in batch_tiles:
-                    nc.vector.tensor_tensor(
-                        out=squashed[GATE_F, m][:], in0=squashed[GATE_F, m][:], in1=c_raw[:, m, :], op=ALU.mult
-                    )
-            if gate == GATE_G:
-                halfway = []
-                for m in batch_tiles:
-                    cell = squashed[GATE_I, m]
-                    nc.vector.tensor_tensor(out=cell[:], in0=cell[:], in1=squashed[GATE_G, m][:], op=ALU.mult)
-                    total = stat.tile([P, 1], F32, tag="total")
-                    nc.vector.scalar_tensor_tensor(
-                        out=cell[:], in0=cell[:], scalar=1.0, in1=squashed[GATE_F, m][:], op0=ALU.mult, op1=ALU.add,
-                        accum_out=total[:],
-                    )
-                    halfway.append(norm_first_half(nc, work, stat, half, cell[:], total, spread[:, ROW_CELL_GAMMA, :]))
-                tanh_c = []
-                for m in batch_tiles:
-                    centred, root = halfway[m]
-                    new_c = acts.tile([P, H], F32, name="new_c%d" % m)
-                    norm_second_half(nc, stat, centred, root, spread[:, ROW_CELL_BETA, :], new_c[:])
-                    nc.sync.dma_start(out=out_1[m * P : (m + 1) * P, :], in_=new_c[:])
-                    tanh_c.append(acts.tile([P, H], F32, name="tanh_c%d" % m))
-                    nc.scalar.activation(out=tanh_c[m][:], in_=new_c[:], func=ACT.Tanh)
-            if gate == GATE_O:
-                for m in batch_tiles:
-                    nc.vector.tensor_tensor(out=tanh_c[m][:], in0=tanh_c[m][:], in1=squashed[GATE_O, m][:], op=ALU.mult)
-                    nc.sync.dma_start(out=out_0[m * P : (m + 1) * P, :], in_=tanh_c[m][:])
+        cell = [squashed[GATE_I, m] for m in batch_tiles]
+        minus_mean = [stat.tile([P, 1], F32, tag="minus_mean", name="minus_mean%d" % m) for m in batch_tiles]
+        for m in batch_tiles:
+            kept = squashed[GATE_F, m]
+            nc.gpsimd.tensor_tensor(out=kept[:], in0=kept[:], in1=c_raw[:, m, :], op=ALU.mult)
+            nc.gpsimd.tensor_tensor(out=cell[m][:], in0=cell[m][:], in1=squashed[GATE_G, m][:], op=ALU.mult)
+        for m in batch_tiles:
+            total = stat.tile([P, 1], F32, tag="total")
+            nc.vector.scalar_tensor_tensor(
+                out=cell[m][:], in0=cell[m][:], scalar=1.0, in1=squashed[GATE_F, m][:], op0=ALU.mult, op1=ALU.add,
+                accum_out=total[:],
+            )
+            nc.vector.tensor_scalar(out=minus_mean[m][:], in0=total[:], scalar1=-1.0 / H, scalar2=None, op0=ALU.mult)
+        halfway = [
+            norm_first_half(nc, work, stat, half, cell[m][:], minus_mean[m], cell_gamma_beta[:, 0, :]) for m in batch_tiles
+        ]
+        for m in batch_tiles:
+            centred, root = halfway[m]
+            inverse = norm_second_half(nc, stat, centred, root, cell_gamma_beta[:, 1, :])
+            tanh_c = acts.tile([P, H], F32, name="tanh_c%d" % m)
+            nc.scalar.activation(out=tanh_c[:], in_=centred[:], func=ACT.Tanh, scale=inverse[:])
+            new_c = acts.tile([P, H], F32, name="new_c%d" % m)
+            nc.scalar.activation(out=new_c[:], in_=centred[:], func=ACT.Copy, scale=inverse[:])
+            nc.sync.dma_start(out=out_1[m * P : (m + 1) * P, :], in_=new_c[:])
+            nc.vector.tensor_tensor(out=tanh_c[:], in0=tanh_c[:], in1=squashed[GATE_O, m][:], op=ALU.mult)
+            nc.sync.dma_start(out=out_0[m * P : (m + 1) * P, :], in_=tanh_c[:])

@@ -136,6 +136,19 @@ def tile_hyperlstmcell_pb_k_kernel(
 
             planes = keep.tile([P, PLANE_TILES + 1, GATES * H], U8, align_bytes=64)
             nc.vector.memset(planes[:].rearrange("p j n -> p (j n)").bitcast(I32), 0)
+            for quad in range(4):
+                nc.gpsimd.dma_start(
+                    out=planes[32 * quad : 32 * quad + 4, PLANE_TILES, :].bitcast(F32),
+                    in_=Whh_scales[0, 4 * quad : 4 * quad + 4, :].bitcast(F32),
+                )
+            for j in range(PLANE_TILES):
+                for quad in range(4):
+                    nc.gpsimd.dma_start(
+                        out=planes[32 * quad : 32 * quad + 16, j, :].bitcast(F32),
+                        in_=Wih_scales[
+                            PLANES_PER_TILE * j : PLANES_PER_TILE * (j + 1), 4 * quad : 4 * quad + 4, :
+                        ].bitcast(F32),
+                    )
 
             with tc.tile_pool(name="raw", bufs=1) as raw:
                 nc.sync.dma_start(out=rows[ROW_GAMMA : ROW_GAMMA + GATES, :], in_=ln_gamma)
@@ -162,19 +175,6 @@ def tile_hyperlstmcell_pb_k_kernel(
                     x_chunk = ring.tile([P, M_TILES, x_cols], BF16, tag="slot", name="x_raw%d" % j, align_bytes=64)
                     nc.sync.dma_start(out=x_chunk[:], in_=x_by_tile[:, :, j * x_cols : (j + 1) * x_cols])
                     x_raw.append(x_chunk)
-                for quad in range(4):
-                    nc.sync.dma_start(
-                        out=planes[32 * quad : 32 * quad + 4, PLANE_TILES, :].bitcast(I32),
-                        in_=Whh_scales[0, 4 * quad : 4 * quad + 4, :].bitcast(I32),
-                    )
-                for j in range(PLANE_TILES):
-                    for quad in range(4):
-                        nc.sync.dma_start(
-                            out=planes[32 * quad : 32 * quad + 16, j, :].bitcast(I32),
-                            in_=Wih_scales[
-                                PLANES_PER_TILE * j : PLANES_PER_TILE * (j + 1), 4 * quad : 4 * quad + 4, :
-                            ].bitcast(I32),
-                        )
                 whh = keep.tile([P, GATES * H * PACK], U8, align_bytes=64)
                 nc.sync.dma_start(out=whh[:].bitcast(I32), in_=Whh_words[0].rearrange("p n t -> p (n t)").bitcast(I32))
                 c_raw = keep.tile([P, M_TILES, H], BF16)

@@ -24,9 +24,10 @@ PLANES_PER_TILE = 4
 PLANE_TILES = X_PASSES // PLANES_PER_TILE
 X_CHUNKS = 4
 PASSES_PER_CHUNK = X_PASSES // X_CHUNKS
-W_TILES_PER_GATE = PLANE_TILES
-PASSES_PER_LOAD = 2
 RING = 8
+SLOT_PASSES = 4
+STAGES = ((GATE_I, GATE_F), (GATE_G,), (GATE_O,))
+LOADS_PER_SLOT = 2
 EPS = 1e-6
 
 FLOPS = 2 * BATCH * (IN + H) * GATES * H + 3 * 2 * BATCH * GATES * H * E
@@ -136,71 +137,78 @@ def tile_hyperlstmcell_pb_k_kernel(
 
             planes = keep.tile([P, PLANE_TILES + 1, GATES * H], U8, align_bytes=64)
             nc.vector.memset(planes[:].rearrange("p j n -> p (j n)").bitcast(I32), 0)
-            for quad in range(4):
-                nc.gpsimd.dma_start(
-                    out=planes[32 * quad : 32 * quad + 4, PLANE_TILES, :].bitcast(F32),
-                    in_=Whh_scales[0, 4 * quad : 4 * quad + 4, :].bitcast(F32),
-                )
-            for j in range(PLANE_TILES):
-                for quad in range(4):
-                    nc.gpsimd.dma_start(
-                        out=planes[32 * quad : 32 * quad + 16, j, :].bitcast(F32),
-                        in_=Wih_scales[
-                            PLANES_PER_TILE * j : PLANES_PER_TILE * (j + 1), 4 * quad : 4 * quad + 4, :
-                        ].bitcast(F32),
-                    )
 
             with tc.tile_pool(name="raw", bufs=1) as raw:
-                nc.sync.dma_start(out=rows[ROW_GAMMA : ROW_GAMMA + GATES, :], in_=ln_gamma)
-                nc.sync.dma_start(out=rows[ROW_BETA : ROW_BETA + GATES, :], in_=ln_beta)
-                nc.sync.dma_start(out=rows[ROW_BIAS : ROW_BIAS + GATES, :], in_=bias.rearrange("(g n) -> g n", g=GATES))
-                nc.sync.dma_start(out=rows[ROW_CELL_GAMMA : ROW_CELL_GAMMA + 1, :], in_=lnc_gamma.rearrange("(o n) -> o n", o=1))
-                nc.sync.dma_start(out=rows[ROW_CELL_BETA : ROW_CELL_BETA + 1, :], in_=lnc_beta.rearrange("(o n) -> o n", o=1))
                 emb_raw = {}
                 ws_raw = {}
                 for which, emb, ws in (("x", emb_x, Wsx), ("h", emb_h, Wsh), ("b", emb_b, Wsb)):
                     emb_raw[which] = raw.tile([P, M_TILES, GATES * E], BF16, name="emb_raw_" + which)
-                    nc.sync.dma_start(out=emb_raw[which][:], in_=emb.rearrange("(m p) g e -> p m (g e)", p=P))
+                    nc.sync.dma_start(out=emb_raw[which][:], in_=emb.rearrange("(p m) g e -> p m (g e)", m=M_TILES))
                     ws_raw[which] = raw.tile([P, GATES, PACK, E], BF16, name="ws_raw_" + which)
                     nc.sync.dma_start(
                         out=ws_raw[which][:].rearrange("q g t e -> q g (t e)"),
                         in_=ws.rearrange("g (q t) e -> q g (t e)", t=PACK),
                     )
+                nc.sync.dma_start(out=rows[ROW_GAMMA : ROW_GAMMA + GATES, :], in_=ln_gamma)
+                nc.sync.dma_start(out=rows[ROW_BETA : ROW_BETA + GATES, :], in_=ln_beta)
+                nc.sync.dma_start(out=rows[ROW_BIAS : ROW_BIAS + GATES, :], in_=bias.rearrange("(g n) -> g n", g=GATES))
+                nc.sync.dma_start(out=rows[ROW_CELL_GAMMA : ROW_CELL_GAMMA + 1, :], in_=lnc_gamma.rearrange("(o n) -> o n", o=1))
+                nc.sync.dma_start(out=rows[ROW_CELL_BETA : ROW_CELL_BETA + 1, :], in_=lnc_beta.rearrange("(o n) -> o n", o=1))
                 h_raw = raw.tile([P, M_TILES, H], BF16)
-                nc.sync.dma_start(out=h_raw[:], in_=h.rearrange("(m p) k -> p m k", p=P))
-                x_by_tile = x.rearrange("(m p) k -> p m k", p=P)
+                nc.sync.dma_start(out=h_raw[:], in_=h.rearrange("(p m) k -> p m k", m=M_TILES))
+                x_by_tile = x.rearrange("(p m) k -> p m k", m=M_TILES)
                 x_cols = PASSES_PER_CHUNK * K_PASS
                 x_raw = []
                 for j in range(X_CHUNKS):
                     x_chunk = ring.tile([P, M_TILES, x_cols], BF16, tag="slot", name="x_raw%d" % j, align_bytes=64)
                     nc.sync.dma_start(out=x_chunk[:], in_=x_by_tile[:, :, j * x_cols : (j + 1) * x_cols])
                     x_raw.append(x_chunk)
+                for quad in range(4):
+                    nc.sync.dma_start(
+                        out=planes[32 * quad : 32 * quad + 4, PLANE_TILES, :].bitcast(I32),
+                        in_=Whh_scales[0, 4 * quad : 4 * quad + 4, :].bitcast(I32),
+                    )
+                for j in range(PLANE_TILES):
+                    for quad in range(4):
+                        nc.sync.dma_start(
+                            out=planes[32 * quad : 32 * quad + 16, j, :].bitcast(I32),
+                            in_=Wih_scales[
+                                PLANES_PER_TILE * j : PLANES_PER_TILE * (j + 1), 4 * quad : 4 * quad + 4, :
+                            ].bitcast(I32),
+                        )
                 whh = keep.tile([P, GATES * H * PACK], U8, align_bytes=64)
                 nc.sync.dma_start(out=whh[:].bitcast(I32), in_=Whh_words[0].rearrange("p n t -> p (n t)").bitcast(I32))
                 c_raw = keep.tile([P, M_TILES, H], BF16)
-                nc.sync.dma_start(out=c_raw[:], in_=c.rearrange("(m p) k -> p m k", p=P))
+                nc.sync.dma_start(out=c_raw[:], in_=c.rearrange("(p m) k -> p m k", m=M_TILES))
 
                 wih_bytes = Wih_words.rearrange("g p n t -> p g (n t)")
                 w_loaded = {}
 
+                w_tiles = [
+                    (stage, first_pass)
+                    for stage, gates in enumerate(STAGES)
+                    for first_pass in range(0, X_PASSES, SLOT_PASSES // len(gates))
+                ]
+
                 def load_weights(index):
-                    gate, j = divmod(index, W_TILES_PER_GATE)
-                    w = ring.tile([P, PLANES_PER_TILE, H * PACK], U8, tag="slot", name="w%d" % index, align_bytes=64)
-                    for first in range(0, PLANES_PER_TILE, PASSES_PER_LOAD):
-                        g = PLANES_PER_TILE * j + first
+                    stage, first_pass = w_tiles[index]
+                    gates = STAGES[stage]
+                    passes = SLOT_PASSES // len(gates)
+                    per_load = passes // LOADS_PER_SLOT
+                    w = ring.tile([P, passes, len(gates) * H * PACK], U8, tag="slot", name="w%d" % index, align_bytes=64)
+                    for i in range(0, passes, per_load):
                         nc.sync.dma_start(
-                            out=w[:, first : first + PASSES_PER_LOAD, :].bitcast(I32),
-                            in_=wih_bytes[:, g : g + PASSES_PER_LOAD, gate * H * PACK : (gate + 1) * H * PACK].bitcast(I32),
+                            out=w[:, i : i + per_load, :].bitcast(I32),
+                            in_=wih_bytes[
+                                :,
+                                first_pass + i : first_pass + i + per_load,
+                                gates[0] * H * PACK : (gates[-1] + 1) * H * PACK,
+                            ].bitcast(I32),
                         )
                     w_loaded[index] = w
 
                 for index in range(RING - X_CHUNKS):
                     load_weights(index)
-
-                bias_all = keep.tile([P, GATES, H], BF16)
-                for gate in range(0, GATES, 2):
-                    both = spread_rows(nc, banks, ident_bf16, rows, (ROW_BIAS + gate, ROW_BIAS + gate + 1))
-                    nc.scalar.copy(out=bias_all[:, gate : gate + 2, :], in_=both[:])
 
                 emb_t = {}
                 ws_t = {}
@@ -247,6 +255,11 @@ def tile_hyperlstmcell_pb_k_kernel(
                     nc.vector.tensor_copy,
                 )
 
+                bias_all = keep.tile([P, GATES, H], BF16)
+                for gate in range(0, GATES, 2):
+                    both = spread_rows(nc, banks, ident_bf16, rows, (ROW_BIAS + gate, ROW_BIAS + gate + 1))
+                    nc.scalar.copy(out=bias_all[:, gate : gate + 2, :], in_=both[:])
+
                 assert X_CHUNKS == GATES
                 x_codes = keep.tile([P, X_PASSES, BATCH], U32, align_bytes=64)
                 x_scales = keep.tile([P, X_PASSES, BATCH], U8, align_bytes=64)
@@ -286,81 +299,96 @@ def tile_hyperlstmcell_pb_k_kernel(
 
             work = ctx.enter_context(tc.tile_pool(name="work", bufs=4, reuse_waits="tile"))
             acts = ctx.enter_context(tc.tile_pool(name="acts", bufs=1, reuse_waits="tile"))
+            tiles = [(gate, m) for gate in range(GATES) for m in batch_tiles]
+            for gate, m in tiles:
+                hh = banks.tile([P, H], F32, tag="bank")
+                nc.tensor.matmul_mx(
+                    out=hh[:],
+                    lhsT=h_codes[:, 0, m * P : (m + 1) * P].bitcast(FP8X4),
+                    lhsT_scale=h_scales[:, 0, m * P : (m + 1) * P],
+                    rhs=whh[:, gate * H * PACK : (gate + 1) * H * PACK].bitcast(FP8X4),
+                    rhs_scale=planes[:, PLANE_TILES, gate * H : (gate + 1) * H],
+                    start=True,
+                    stop=True,
+                )
+                nc.vector.tensor_tensor(out=zh[gate, m][:], in0=hh[:], in1=zh[gate, m][:], op=ALU.mult)
             rest_sum = {}
-            for gate in range(GATES):
-                for m in batch_tiles:
-                    hh = banks.tile([P, H], F32, tag="bank")
-                    nc.tensor.matmul_mx(
-                        out=hh[:],
-                        lhsT=h_codes[:, 0, m * P : (m + 1) * P].bitcast(FP8X4),
-                        lhsT_scale=h_scales[:, 0, m * P : (m + 1) * P],
-                        rhs=whh[:, gate * H * PACK : (gate + 1) * H * PACK].bitcast(FP8X4),
-                        rhs_scale=planes[:, PLANE_TILES, gate * H : (gate + 1) * H],
-                        start=True,
-                        stop=True,
-                    )
-                    nc.vector.tensor_tensor(out=zh[gate, m][:], in0=hh[:], in1=zh[gate, m][:], op=ALU.mult)
-                    nc.gpsimd.tensor_tensor(out=rest[gate, m][:], in0=rest[gate, m][:], in1=zh[gate, m][:], op=ALU.add)
-                    unused = work.tile([P, H], F32, tag="squares")
-                    rest_sum[gate, m] = keep.tile([P, 1], F32, name="rest_sum%d_%d" % (gate, m))
-                    nc.scalar.activation(out=unused[:], in_=rest[gate, m][:], func=ACT.Copy, accum_out=rest_sum[gate, m][:])
+            for gate, m in tiles:
+                rest_sum[gate, m] = keep.tile([P, 1], F32, name="rest_sum%d_%d" % (gate, m))
+                nc.vector.scalar_tensor_tensor(
+                    out=rest[gate, m][:], in0=rest[gate, m][:], scalar=1.0, in1=zh[gate, m][:], op0=ALU.mult, op1=ALU.add,
+                    accum_out=rest_sum[gate, m][:],
+                )
 
         squashed = {}
-        for gate in range(GATES):
-            gamma_beta = spread_rows(nc, banks, ident_bf16, rows, (ROW_GAMMA + gate, ROW_BETA + gate))
-            if gate == GATE_O:
+        index = 0
+        for gates in STAGES:
+            gamma_beta = {}
+            xh = {}
+            for gate in gates:
+                gamma_beta[gate] = spread_rows(nc, banks, ident_bf16, rows, (ROW_GAMMA + gate, ROW_BETA + gate))
+                for m in batch_tiles:
+                    xh[gate, m] = banks.tile([P, H], F32, tag="bank", name="xh%d_%d" % (gate, m))
+            if GATE_O in gates:
                 cell_gamma_beta = spread_rows(nc, banks, ident_bf16, rows, (ROW_CELL_GAMMA, ROW_CELL_BETA))
-            xh = [banks.tile([P, H], F32, tag="bank", name="xh%d_%d" % (gate, m)) for m in batch_tiles]
-            for j in range(W_TILES_PER_GATE):
-                index = gate * W_TILES_PER_GATE + j
-                for first in range(0, PLANES_PER_TILE, PASSES_PER_LOAD):
-                    for m in batch_tiles:
-                        for i in range(first, first + PASSES_PER_LOAD):
-                            g = PLANES_PER_TILE * j + i
-                            nc.tensor.matmul_mx(
-                                out=xh[m][:],
-                                lhsT=x_codes[:, g, m * P : (m + 1) * P].bitcast(FP8X4),
-                                lhsT_scale=x_scales[:, g, m * P : (m + 1) * P],
-                                rhs=w_loaded[index][:, i, :].bitcast(FP8X4),
-                                rhs_scale=planes[4 * i : P, j, gate * H : (gate + 1) * H],
-                                start=(g == 0),
-                                stop=(g == X_PASSES - 1),
-                            )
-                if index + RING < GATES * W_TILES_PER_GATE:
+            passes = SLOT_PASSES // len(gates)
+            per_load = passes // LOADS_PER_SLOT
+            for first_pass in range(0, X_PASSES, passes):
+                for first in range(0, passes, per_load):
+                    for position, gate in enumerate(gates):
+                        for m in batch_tiles:
+                            for i in range(first, first + per_load):
+                                g = first_pass + i
+                                nc.tensor.matmul_mx(
+                                    out=xh[gate, m][:],
+                                    lhsT=x_codes[:, g, m * P : (m + 1) * P].bitcast(FP8X4),
+                                    lhsT_scale=x_scales[:, g, m * P : (m + 1) * P],
+                                    rhs=w_loaded[index][:, i, position * H * PACK : (position + 1) * H * PACK].bitcast(FP8X4),
+                                    rhs_scale=planes[
+                                        4 * (g % PLANES_PER_TILE) : P, g // PLANES_PER_TILE, gate * H : (gate + 1) * H
+                                    ],
+                                    start=(g == 0),
+                                    stop=(g == X_PASSES - 1),
+                                )
+                if index + RING < len(w_tiles):
                     load_weights(index + RING)
+                index += 1
 
-            pre = [work.tile([P, H], F32, tag="pre", name="pre%d" % m) for m in batch_tiles]
-            minus_mean = [stat.tile([P, 1], F32, tag="minus_mean", name="minus_mean%d" % m) for m in batch_tiles]
-            for m in batch_tiles:
-                product_sum = stat.tile([P, 1], F32, tag="product_sum")
-                nc.vector.scalar_tensor_tensor(
-                    out=pre[m][:], in0=xh[m][:], scalar=1.0, in1=zx[gate, m][:], op0=ALU.mult, op1=ALU.mult,
-                    accum_out=product_sum[:],
-                )
-                nc.vector.tensor_scalar(
-                    out=minus_mean[m][:], in0=product_sum[:], scalar1=rest_sum[gate, m][:], scalar2=-1.0 / H,
-                    op0=ALU.add, op1=ALU.mult,
-                )
-            for m in batch_tiles:
-                nc.vector.tensor_tensor(out=pre[m][:], in0=pre[m][:], in1=rest[gate, m][:], op=ALU.add)
-            halfway = [
-                norm_first_half(nc, work, stat, half, pre[m][:], minus_mean[m], gamma_beta[:, 0, :]) for m in batch_tiles
-            ]
-            for m in batch_tiles:
-                centred, root = halfway[m]
-                inverse = norm_second_half(nc, stat, centred, root, gamma_beta[:, 1, :])
-                squashed[gate, m] = acts.tile([P, H], F32, name="squashed%d_%d" % (gate, m))
-                nc.scalar.activation(
-                    out=squashed[gate, m][:], in_=centred[:], func=(ACT.Tanh if gate == GATE_G else ACT.Sigmoid),
-                    scale=inverse[:],
-                )
+            for gate in gates:
+                pre = [work.tile([P, H], F32, tag="pre", name="pre%d" % m) for m in batch_tiles]
+                minus_mean = [stat.tile([P, 1], F32, tag="minus_mean", name="minus_mean%d" % m) for m in batch_tiles]
+                for m in batch_tiles:
+                    product_sum = stat.tile([P, 1], F32, tag="product_sum")
+                    nc.vector.scalar_tensor_tensor(
+                        out=pre[m][:], in0=xh[gate, m][:], scalar=1.0, in1=zx[gate, m][:], op0=ALU.mult, op1=ALU.mult,
+                        accum_out=product_sum[:],
+                    )
+                    nc.vector.tensor_scalar(
+                        out=minus_mean[m][:], in0=product_sum[:], scalar1=rest_sum[gate, m][:], scalar2=-1.0 / H,
+                        op0=ALU.add, op1=ALU.mult,
+                    )
+                for m in batch_tiles:
+                    nc.vector.tensor_tensor(out=pre[m][:], in0=pre[m][:], in1=rest[gate, m][:], op=ALU.add)
+                halfway = [
+                    norm_first_half(nc, work, stat, half, pre[m][:], minus_mean[m], gamma_beta[gate][:, 0, :])
+                    for m in batch_tiles
+                ]
+                for m in batch_tiles:
+                    centred, root = halfway[m]
+                    inverse = norm_second_half(nc, stat, centred, root, gamma_beta[gate][:, 1, :])
+                    squashed[gate, m] = acts.tile([P, H], F32, name="squashed%d_%d" % (gate, m))
+                    nc.scalar.activation(
+                        out=squashed[gate, m][:], in_=centred[:], func=(ACT.Tanh if gate == GATE_G else ACT.Sigmoid),
+                        scale=inverse[:],
+                    )
 
         cell = [squashed[GATE_I, m] for m in batch_tiles]
         minus_mean = [stat.tile([P, 1], F32, tag="minus_mean", name="minus_mean%d" % m) for m in batch_tiles]
         for m in batch_tiles:
             kept = squashed[GATE_F, m]
-            nc.gpsimd.tensor_tensor(out=kept[:], in0=kept[:], in1=c_raw[:, m, :], op=ALU.mult)
-            nc.gpsimd.tensor_tensor(out=cell[m][:], in0=cell[m][:], in1=squashed[GATE_G, m][:], op=ALU.mult)
+            nc.vector.tensor_tensor(out=kept[:], in0=kept[:], in1=c_raw[:, m, :], op=ALU.mult)
+        for m in batch_tiles:
+            nc.vector.tensor_tensor(out=cell[m][:], in0=cell[m][:], in1=squashed[GATE_G, m][:], op=ALU.mult)
         for m in batch_tiles:
             total = stat.tile([P, 1], F32, tag="total")
             nc.vector.scalar_tensor_tensor(
@@ -378,6 +406,6 @@ def tile_hyperlstmcell_pb_k_kernel(
             nc.scalar.activation(out=tanh_c[:], in_=centred[:], func=ACT.Tanh, scale=inverse[:])
             new_c = acts.tile([P, H], F32, name="new_c%d" % m)
             nc.scalar.activation(out=new_c[:], in_=centred[:], func=ACT.Copy, scale=inverse[:])
-            nc.sync.dma_start(out=out_1[m * P : (m + 1) * P, :], in_=new_c[:])
+            nc.sync.dma_start(out=out_1.rearrange("(p m) n -> p m n", m=M_TILES)[:, m, :], in_=new_c[:])
             nc.vector.tensor_tensor(out=tanh_c[:], in0=tanh_c[:], in1=squashed[GATE_O, m][:], op=ALU.mult)
-            nc.sync.dma_start(out=out_0[m * P : (m + 1) * P, :], in_=tanh_c[:])
+            nc.sync.dma_start(out=out_0.rearrange("(p m) n -> p m n", m=M_TILES)[:, m, :], in_=tanh_c[:])

@@ -26,7 +26,7 @@ X_CHUNKS = 4
 PASSES_PER_CHUNK = X_PASSES // X_CHUNKS
 RING = 8
 SLOT_PASSES = 4
-STAGES = ((GATE_I, GATE_F), (GATE_G,), (GATE_O,))
+STAGES = ((GATE_G,), (GATE_I,), (GATE_F,), (GATE_O,))
 LOADS_PER_SLOT = 2
 EPS = 1e-6
 

@@ -19,6 +19,7 @@ GATE_I, GATE_F, GATE_G, GATE_O = 0, 1, 2, 3
 M_TILES = BATCH // P
 PACK = 4
 K_PASS = P * PACK
+UNITS_PER_ROW = GATES * H // P
 X_PASSES = IN // K_PASS
 PLANES_PER_TILE = 4
 PLANE_TILES = X_PASSES // PLANES_PER_TILE
@@ -36,11 +37,11 @@ ROW_GAMMA, ROW_BETA, ROW_BIAS, ROW_CELL_GAMMA, ROW_CELL_BETA = 0, 4, 8, 12, 13
 
 
 def units_in_order(ap):
-    return ap.rearrange("b (t q) -> b q t", t=PACK)
+    return ap.rearrange("b (t q) -> b q t", t=UNITS_PER_ROW)
 
 
 def units_as_pairs(ap):
-    return ap.rearrange("b (q t) -> b q t", t=PACK)
+    return ap.rearrange("b (q t) -> b q t", t=UNITS_PER_ROW)
 
 
 def flip_pass(nc, banks, words, g, ident_f32, grouped, engine_copy):
@@ -144,10 +145,10 @@ def tile_hyperlstmcell_pb_k_kernel(
                 for which, emb, ws in (("x", emb_x, Wsx), ("h", emb_h, Wsh), ("b", emb_b, Wsb)):
                     emb_raw[which] = raw.tile([P, M_TILES, GATES * E], BF16, name="emb_raw_" + which)
                     nc.sync.dma_start(out=emb_raw[which][:], in_=emb.rearrange("(p m) g e -> p m (g e)", m=M_TILES))
-                    ws_raw[which] = raw.tile([P, GATES, PACK, E], BF16, name="ws_raw_" + which)
+                    ws_raw[which] = raw.tile([P, UNITS_PER_ROW, E], BF16, name="ws_raw_" + which)
                     nc.sync.dma_start(
-                        out=ws_raw[which][:].rearrange("q g t e -> q g (t e)"),
-                        in_=ws.rearrange("g (q t) e -> q g (t e)", t=PACK),
+                        out=ws_raw[which][:].rearrange("p t e -> p (t e)"),
+                        in_=ws.rearrange("g (q t) e -> (g q) (t e)", t=UNITS_PER_ROW),
                     )
                 nc.sync.dma_start(out=rows[ROW_GAMMA : ROW_GAMMA + GATES, :], in_=ln_gamma)
                 nc.sync.dma_start(out=rows[ROW_BETA : ROW_BETA + GATES, :], in_=ln_beta)
@@ -190,11 +191,14 @@ def tile_hyperlstmcell_pb_k_kernel(
                     for first_pass in range(0, X_PASSES, SLOT_PASSES // len(gates))
                 ]
 
+                def passes_per_load(index):
+                    return 1 if index == len(w_tiles) - 1 else SLOT_PASSES // LOADS_PER_SLOT
+
                 def load_weights(index):
                     stage, first_pass = w_tiles[index]
                     gates = STAGES[stage]
                     passes = SLOT_PASSES // len(gates)
-                    per_load = passes // LOADS_PER_SLOT
+                    per_load = passes_per_load(index)
                     w = ring.tile([P, passes, len(gates) * H * PACK], U8, tag="slot", name="w%d" % index, align_bytes=64)
                     for i in range(0, passes, per_load):
                         nc.sync.dma_start(
@@ -229,12 +233,16 @@ def tile_hyperlstmcell_pb_k_kernel(
                             in_=flipped[:].rearrange("e g m b -> e (g m b)"),
                         )
                     ws_t[which] = raw.tile([P, GATES, H], BF16, name="ws_t_" + which)
-                    for gate in range(GATES):
-                        flipped = banks.tile([P, PACK, P], BF16, tag="bank")
-                        for t in range(PACK):
-                            nc.tensor.transpose(flipped[:, t, :], ws_raw[which][:, gate, t, :], ident_bf16[:])
-                        copy = nc.vector.tensor_copy if gate % 2 == 0 else nc.scalar.copy
-                        copy(out=ws_t[which][:, gate, :], in_=flipped[:].rearrange("e t q -> e (t q)"))
+                    per_bank = 4
+                    for first in range(0, UNITS_PER_ROW, per_bank):
+                        flipped = banks.tile([P, per_bank, P], BF16, tag="bank")
+                        for t in range(per_bank):
+                            nc.tensor.transpose(flipped[:, t, :], ws_raw[which][:, first + t, :], ident_bf16[:])
+                        copy = nc.vector.tensor_copy if (first // per_bank) % 2 == 0 else nc.scalar.copy
+                        copy(
+                            out=ws_t[which][:].rearrange("e g (t q) -> e g t q", t=UNITS_PER_ROW)[:, :, first : first + per_bank, :],
+                            in_=flipped[:].rearrange("e t (g q) -> e g t q", g=GATES),
+                        )
 
                 def expand(which, gate, m):
                     z = banks.tile([P, H], F32, tag="bank")
@@ -312,12 +320,16 @@ def tile_hyperlstmcell_pb_k_kernel(
                     stop=True,
                 )
                 nc.vector.tensor_tensor(out=zh[gate, m][:], in0=hh[:], in1=zh[gate, m][:], op=ALU.mult)
-            rest_sum = {}
+            minus_rest_mean = {}
             for gate, m in tiles:
-                rest_sum[gate, m] = keep.tile([P, 1], F32, name="rest_sum%d_%d" % (gate, m))
+                rest_sum = stat.tile([P, 1], F32, tag="rest_sum")
                 nc.vector.scalar_tensor_tensor(
                     out=rest[gate, m][:], in0=rest[gate, m][:], scalar=1.0, in1=zh[gate, m][:], op0=ALU.mult, op1=ALU.add,
-                    accum_out=rest_sum[gate, m][:],
+                    accum_out=rest_sum[:],
+                )
+                minus_rest_mean[gate, m] = keep.tile([P, 1], F32, name="minus_rest_mean%d_%d" % (gate, m))
+                nc.gpsimd.tensor_scalar(
+                    out=minus_rest_mean[gate, m][:], in0=rest_sum[:], scalar1=-1.0 / H, scalar2=0.0, op0=ALU.mult, op1=ALU.add
                 )
 
         squashed = {}
@@ -332,8 +344,8 @@ def tile_hyperlstmcell_pb_k_kernel(
             if GATE_O in gates:
                 cell_gamma_beta = spread_rows(nc, banks, ident_bf16, rows, (ROW_CELL_GAMMA, ROW_CELL_BETA))
             passes = SLOT_PASSES // len(gates)
-            per_load = passes // LOADS_PER_SLOT
             for first_pass in range(0, X_PASSES, passes):
+                per_load = passes_per_load(index)
                 for first in range(0, passes, per_load):
                     for position, gate in enumerate(gates):
                         for m in batch_tiles:
@@ -363,9 +375,9 @@ def tile_hyperlstmcell_pb_k_kernel(
                         out=pre[m][:], in0=xh[gate, m][:], scalar=1.0, in1=zx[gate, m][:], op0=ALU.mult, op1=ALU.mult,
                         accum_out=product_sum[:],
                     )
-                    nc.vector.tensor_scalar(
-                        out=minus_mean[m][:], in0=product_sum[:], scalar1=rest_sum[gate, m][:], scalar2=-1.0 / H,
-                        op0=ALU.add, op1=ALU.mult,
+                    nc.scalar.activation(
+                        out=minus_mean[m][:], in_=product_sum[:], func=ACT.Identity, scale=-1.0 / H,
+                        bias=minus_rest_mean[gate, m][:],
                     )
                 for m in batch_tiles:
                     nc.vector.tensor_tensor(out=pre[m][:], in0=pre[m][:], in1=rest[gate, m][:], op=ALU.add)
@@ -395,7 +407,7 @@ def tile_hyperlstmcell_pb_k_kernel(
                 out=cell[m][:], in0=cell[m][:], scalar=1.0, in1=squashed[GATE_F, m][:], op0=ALU.mult, op1=ALU.add,
                 accum_out=total[:],
             )
-            nc.vector.tensor_scalar(out=minus_mean[m][:], in0=total[:], scalar1=-1.0 / H, scalar2=None, op0=ALU.mult)
+            nc.scalar.mul(out=minus_mean[m][:], in_=total[:], mul=-1.0 / H)
         halfway = [
             norm_first_half(nc, work, stat, half, cell[m][:], minus_mean[m], cell_gamma_beta[:, 0, :]) for m in batch_tiles
         ]

@@ -179,8 +179,6 @@ def tile_hyperlstmcell_pb_k_kernel(
                         )
                 whh = keep.tile([P, GATES * H * PACK], U8, align_bytes=64)
                 nc.sync.dma_start(out=whh[:].bitcast(I32), in_=Whh_words[0].rearrange("p n t -> p (n t)").bitcast(I32))
-                c_raw = keep.tile([P, M_TILES, H], BF16)
-                nc.sync.dma_start(out=c_raw[:], in_=c.rearrange("(p m) k -> p m k", m=M_TILES))
 
                 wih_bytes = Wih_words.rearrange("g p n t -> p g (n t)")
                 w_loaded = {}
@@ -332,9 +330,13 @@ def tile_hyperlstmcell_pb_k_kernel(
                     out=minus_rest_mean[gate, m][:], in0=rest_sum[:], scalar1=-1.0 / H, scalar2=0.0, op0=ALU.mult, op1=ALU.add
                 )
 
+        ctx.enter_context(tc.manual_schedule(engines={mybir.EngineType.SP}))
         squashed = {}
         index = 0
         for gates in STAGES:
+            if gates == STAGES[-3]:
+                c_raw = keep.tile([P, M_TILES, H], BF16)
+                nc.sync.dma_start(out=c_raw[:], in_=c.rearrange("(p m) k -> p m k", m=M_TILES))
             gamma_beta = {}
             xh = {}
             for gate in gates:

@@ -29,6 +29,7 @@ RING = 8
 SLOT_PASSES = 4
 STAGES = ((GATE_G,), (GATE_I,), (GATE_F,), (GATE_O,))
 LOADS_PER_SLOT = 2
+TILES_BEFORE_WHH = 2
 EPS = 1e-6
 
 FLOPS = 2 * BATCH * (IN + H) * GATES * H + 3 * 2 * BATCH * GATES * H * E
@@ -177,8 +178,6 @@ def tile_hyperlstmcell_pb_k_kernel(
                                 PLANES_PER_TILE * j : PLANES_PER_TILE * (j + 1), 4 * quad : 4 * quad + 4, :
                             ].bitcast(I32),
                         )
-                whh = keep.tile([P, GATES * H * PACK], U8, align_bytes=64)
-                nc.sync.dma_start(out=whh[:].bitcast(I32), in_=Whh_words[0].rearrange("p n t -> p (n t)").bitcast(I32))
 
                 wih_bytes = Wih_words.rearrange("g p n t -> p g (n t)")
                 w_loaded = {}
@@ -210,6 +209,11 @@ def tile_hyperlstmcell_pb_k_kernel(
                     w_loaded[index] = w
 
                 for index in range(RING - X_CHUNKS):
+                    if index == TILES_BEFORE_WHH:
+                        whh = keep.tile([P, GATES * H * PACK], U8, align_bytes=64)
+                        nc.sync.dma_start(
+                            out=whh[:].bitcast(I32), in_=Whh_words[0].rearrange("p n t -> p (n t)").bitcast(I32)
+                        )
                     load_weights(index)
 
                 emb_t = {}
@@ -305,7 +309,10 @@ def tile_hyperlstmcell_pb_k_kernel(
 
             work = ctx.enter_context(tc.tile_pool(name="work", bufs=4, reuse_waits="tile"))
             acts = ctx.enter_context(tc.tile_pool(name="acts", bufs=1, reuse_waits="tile"))
-            tiles = [(gate, m) for gate in range(GATES) for m in batch_tiles]
+        minus_rest_mean = {}
+
+        def hidden_products():
+            tiles = [(gate, m) for (gate,) in STAGES for m in batch_tiles]
             for gate, m in tiles:
                 hh = banks.tile([P, H], F32, tag="bank")
                 nc.tensor.matmul_mx(
@@ -318,7 +325,6 @@ def tile_hyperlstmcell_pb_k_kernel(
                     stop=True,
                 )
                 nc.vector.tensor_tensor(out=zh[gate, m][:], in0=hh[:], in1=zh[gate, m][:], op=ALU.mult)
-            minus_rest_mean = {}
             for gate, m in tiles:
                 rest_sum = stat.tile([P, 1], F32, tag="rest_sum")
                 nc.vector.scalar_tensor_tensor(
@@ -367,6 +373,8 @@ def tile_hyperlstmcell_pb_k_kernel(
                 if index + RING < len(w_tiles):
                     load_weights(index + RING)
                 index += 1
+                if index == TILES_BEFORE_WHH:
+                    hidden_products()
 
             for gate in gates:
                 pre = [work.tile([P, H], F32, tag="pre", name="pre%d" % m) for m in batch_tiles]

import math
from contextlib import ExitStack

import concourse.mybir as mybir
from concourse.masks import make_identity

F32 = mybir.dt.float32
BF16 = mybir.dt.bfloat16
I32 = mybir.dt.int32
U32 = mybir.dt.uint32
U8 = mybir.dt.uint8
FP8X4 = mybir.dt.float8_e4m3fn_x4
ALU = mybir.AluOpType
ACT = mybir.ActivationFunctionType

P = 128
BATCH, IN, H, E, GATES = 256, 8192, 512, 128, 4
GATE_I, GATE_F, GATE_G, GATE_O = 0, 1, 2, 3
M_TILES = BATCH // P
PACK = 4
K_PASS = P * PACK
UNITS_PER_ROW = GATES * H // P
X_PASSES = IN // K_PASS
PLANES_PER_TILE = 4
PLANE_TILES = X_PASSES // PLANES_PER_TILE
X_CHUNKS = 4
PASSES_PER_CHUNK = X_PASSES // X_CHUNKS
RING = 8
SLOT_PASSES = 4
STAGES = ((GATE_G,), (GATE_I,), (GATE_F,), (GATE_O,))
LOADS_PER_SLOT = 2
TILES_BEFORE_WHH = 2
EPS = 1e-6

FLOPS = 2 * BATCH * (IN + H) * GATES * H + 3 * 2 * BATCH * GATES * H * E

ROW_GAMMA, ROW_BETA, ROW_BIAS, ROW_CELL_GAMMA, ROW_CELL_BETA = 0, 4, 8, 12, 13


def units_in_order(ap):
    return ap.rearrange("b (t q) -> b q t", t=UNITS_PER_ROW)


def units_as_pairs(ap):
    return ap.rearrange("b (q t) -> b q t", t=UNITS_PER_ROW)


def flip_pass(nc, banks, words, g, ident_f32, grouped, engine_copy):
    flipped = banks.tile([P, M_TILES, 2, P], F32, tag="bank")
    for m in range(M_TILES):
        for u in range(2):
            nc.tensor.transpose(flipped[:, m, u, :], words[m][:, 2 * P * g + u : 2 * P * (g + 1) : 2], ident_f32[:])
    side_by_side = grouped.rearrange("p c t -> p (c t)").bitcast(F32).rearrange("p (m b u) -> p m b u", m=M_TILES, u=2)
    engine_copy(out=side_by_side, in_=flipped[:].rearrange("p m u b -> p m b u"))


def spread_rows(nc, banks, ident_bf16, rows, chosen):
    both = banks.tile([P, 2, H], BF16, tag="bank")
    for i, r in enumerate(chosen):
        nc.tensor.matmul(
            both[:, i, :], lhsT=ident_bf16[:, r : r + 1].to_broadcast([P, P]), rhs=rows[:], start=True, stop=True
        )
    return both


def quantise(nc, grouped, codes, scales):
    nc.vector.quantize_mx(
        out=codes.rearrange("p g c -> p (g c)").bitcast(FP8X4),
        scales=scales.rearrange("p g c -> p (g c)"),
        in_=grouped[:].rearrange("p g c t -> p (g c t)"),
    )


def norm_first_half(nc, work, stat, half, values, minus_mean, gamma):
    squares = work.tile([P, H], F32, tag="squares")
    sum_of_squares = stat.tile([P, 1], F32, tag="sum_of_squares")
    nc.scalar.activation(out=squares[:], in_=values, func=ACT.Square, bias=minus_mean[:], accum_out=sum_of_squares[:])
    centred = work.tile([P, H], F32, tag="centred")
    nc.vector.scalar_tensor_tensor(out=centred[:], in0=values, scalar=minus_mean[:], in1=gamma, op0=ALU.add, op1=ALU.mult)
    root = stat.tile([P, 1], F32, tag="root")
    nc.gpsimd.tensor_tensor(out=root[:], in0=sum_of_squares[:], in1=half[:], op=ALU.pow)
    return centred, root


def norm_second_half(nc, stat, centred, root, beta):
    divisor = stat.tile([P, 1], F32, tag="divisor")
    nc.vector.tensor_scalar(
        out=divisor[:], in0=root[:], scalar1=1.0 / math.sqrt(H - 1), scalar2=EPS, op0=ALU.mult, op1=ALU.add
    )
    nc.vector.scalar_tensor_tensor(out=centred[:], in0=beta, scalar=divisor[:], in1=centred[:], op0=ALU.mult, op1=ALU.add)
    inverse = stat.tile([P, 1], F32, tag="inverse")
    nc.vector.reciprocal(out=inverse[:], in_=divisor[:])
    return inverse


def tile_hyperlstmcell_pb_k_kernel(
    tc,
    x,
    h,
    c,
    emb_h,
    emb_x,
    emb_b,
    Wsh,
    Wsx,
    Wsb,
    Wih_words,
    Wih_scales,
    Whh_words,
    Whh_scales,
    bias,
    ln_gamma,
    ln_beta,
    lnc_gamma,
    lnc_beta,
    out_0,
    out_1,
):
    nc = tc.nc
    batch_tiles = range(M_TILES)
    with ExitStack() as ctx:
        keep = ctx.enter_context(tc.tile_pool(name="keep", bufs=1))
        ring = ctx.enter_context(tc.tile_pool(name="ring", bufs=RING))
        stat = ctx.enter_context(tc.tile_pool(name="stat", bufs=4))
        late = ctx.enter_context(tc.tile_pool(name="late", bufs=1))
        banks = ctx.enter_context(tc.psum_pool(name="banks", bufs=8))

        with tc.manual_schedule():
            rows = keep.tile([P, H], BF16)
            nc.vector.memset(rows[:].bitcast(I32), 0)
            half = keep.tile([P, 1], F32)
            nc.vector.memset(half[:], 0.5)
            ident_bf16 = keep.tile([P, P], BF16)
            make_identity(nc, ident_bf16[:])
            ident_f32 = keep.tile([P, P], F32)
            make_identity(nc, ident_f32[:])
            warm = keep.tile([P, 1], F32)
            nc.scalar.activation(out=warm[:], in_=half[:], func=ACT.Sigmoid)

            planes = keep.tile([P, PLANE_TILES + 1, GATES * H], U8, align_bytes=64)
            nc.vector.memset(planes[:].rearrange("p j n -> p (j n)").bitcast(I32), 0)

            with tc.tile_pool(name="raw", bufs=1) as raw:
                emb_raw = {}
                ws_raw = {}
                for which, emb, ws in (("x", emb_x, Wsx), ("h", emb_h, Wsh), ("b", emb_b, Wsb)):
                    emb_raw[which] = raw.tile([P, M_TILES, GATES * E], BF16, name="emb_raw_" + which)
                    nc.sync.dma_start(out=emb_raw[which][:], in_=emb.rearrange("(p m) g e -> p m (g e)", m=M_TILES))
                    ws_raw[which] = raw.tile([P, UNITS_PER_ROW, E], BF16, name="ws_raw_" + which)
                    nc.sync.dma_start(
                        out=ws_raw[which][:].rearrange("p t e -> p (t e)"),
                        in_=ws.rearrange("g (q t) e -> (g q) (t e)", t=UNITS_PER_ROW),
                    )
                nc.sync.dma_start(out=rows[ROW_GAMMA : ROW_GAMMA + GATES, :], in_=ln_gamma)
                nc.sync.dma_start(out=rows[ROW_BETA : ROW_BETA + GATES, :], in_=ln_beta)
                nc.sync.dma_start(out=rows[ROW_BIAS : ROW_BIAS + GATES, :], in_=bias.rearrange("(g n) -> g n", g=GATES))
                nc.sync.dma_start(out=rows[ROW_CELL_GAMMA : ROW_CELL_GAMMA + 1, :], in_=lnc_gamma.rearrange("(o n) -> o n", o=1))
                nc.sync.dma_start(out=rows[ROW_CELL_BETA : ROW_CELL_BETA + 1, :], in_=lnc_beta.rearrange("(o n) -> o n", o=1))
                h_raw = raw.tile([P, M_TILES, H], BF16)
                nc.sync.dma_start(out=h_raw[:], in_=h.rearrange("(p m) k -> p m k", m=M_TILES))
                x_by_tile = x.rearrange("(p m) k -> p m k", m=M_TILES)
                x_cols = PASSES_PER_CHUNK * K_PASS
                x_raw = []
                for j in range(X_CHUNKS):
                    x_chunk = ring.tile([P, M_TILES, x_cols], BF16, tag="slot", name="x_raw%d" % j, align_bytes=64)
                    nc.sync.dma_start(out=x_chunk[:], in_=x_by_tile[:, :, j * x_cols : (j + 1) * x_cols])
                    x_raw.append(x_chunk)
                for quad in range(4):
                    nc.sync.dma_start(
                        out=planes[32 * quad : 32 * quad + 4, PLANE_TILES, :].bitcast(I32),
                        in_=Whh_scales[0, 4 * quad : 4 * quad + 4, :].bitcast(I32),
                    )
                for j in range(PLANE_TILES):
                    for quad in range(4):
                        nc.sync.dma_start(
                            out=planes[32 * quad : 32 * quad + 16, j, :].bitcast(I32),
                            in_=Wih_scales[
                                PLANES_PER_TILE * j : PLANES_PER_TILE * (j + 1), 4 * quad : 4 * quad + 4, :
                            ].bitcast(I32),
                        )

                wih_bytes = Wih_words.rearrange("g p n t -> p g (n t)")
                w_loaded = {}

                w_tiles = [
                    (stage, first_pass)
                    for stage, gates in enumerate(STAGES)
                    for first_pass in range(0, X_PASSES, SLOT_PASSES // len(gates))
                ]

                def passes_per_load(index):
                    return 1 if index == len(w_tiles) - 1 else SLOT_PASSES // LOADS_PER_SLOT

                def load_weights(index):
                    stage, first_pass = w_tiles[index]
                    gates = STAGES[stage]
                    passes = SLOT_PASSES // len(gates)
                    per_load = passes_per_load(index)
                    w = ring.tile([P, passes, len(gates) * H * PACK], U8, tag="slot", name="w%d" % index, align_bytes=64)
                    for i in range(0, passes, per_load):
                        nc.sync.dma_start(
                            out=w[:, i : i + per_load, :].bitcast(I32),
                            in_=wih_bytes[
                                :,
                                first_pass + i : first_pass + i + per_load,
                                gates[0] * H * PACK : (gates[-1] + 1) * H * PACK,
                            ].bitcast(I32),
                        )
                    w_loaded[index] = w

                for index in range(RING - X_CHUNKS):
                    if index == TILES_BEFORE_WHH:
                        whh = keep.tile([P, GATES * H * PACK], U8, align_bytes=64)
                        nc.sync.dma_start(
                            out=whh[:].bitcast(I32), in_=Whh_words[0].rearrange("p n t -> p (n t)").bitcast(I32)
                        )
                    load_weights(index)

                emb_t = {}
                ws_t = {}
                for which in ("x", "h", "b"):
                    emb_t[which] = raw.tile([P, GATES, BATCH], BF16, name="emb_t_" + which)
                    for first in range(0, GATES, 2):
                        flipped = banks.tile([P, 2, M_TILES, P], BF16, tag="bank")
                        for i in range(2):
                            for m in batch_tiles:
                                nc.tensor.transpose(
                                    flipped[:, i, m, :],
                                    emb_raw[which][:, m, (first + i) * E : (first + i + 1) * E],
                                    ident_bf16[:],
                                )
                        copy = nc.vector.tensor_copy if first == 0 else nc.scalar.copy
                        copy(
                            out=emb_t[which][:, first : first + 2, :].rearrange("e g b -> e (g b)"),
                            in_=flipped[:].rearrange("e g m b -> e (g m b)"),
                        )
                    ws_t[which] = raw.tile([P, GATES, H], BF16, name="ws_t_" + which)
                    per_bank = 4
                    for first in range(0, UNITS_PER_ROW, per_bank):
                        flipped = banks.tile([P, per_bank, P], BF16, tag="bank")
                        for t in range(per_bank):
                            nc.tensor.transpose(flipped[:, t, :], ws_raw[which][:, first + t, :], ident_bf16[:])
                        copy = nc.vector.tensor_copy if (first // per_bank) % 2 == 0 else nc.scalar.copy
                        copy(
                            out=ws_t[which][:].rearrange("e g (t q) -> e g t q", t=UNITS_PER_ROW)[:, :, first : first + per_bank, :],
                            in_=flipped[:].rearrange("e t (g q) -> e g t q", g=GATES),
                        )

                def expand(which, gate, m):
                    z = banks.tile([P, H], F32, tag="bank")
                    nc.tensor.matmul(
                        z[:],
                        lhsT=emb_t[which][:, gate, m * P : (m + 1) * P],
                        rhs=ws_t[which][:, gate, :],
                        start=True,
                        stop=True,
                    )
                    return z

                h_codes = keep.tile([P, 1, BATCH], U32, align_bytes=64)
                h_scales = keep.tile([P, 1, BATCH], U8, align_bytes=64)
                h_grouped = raw.tile([P, 1, BATCH, PACK], BF16, align_bytes=64)
                flip_pass(
                    nc, banks, [h_raw[:, m, :].bitcast(F32) for m in batch_tiles], 0, ident_f32, h_grouped[:, 0],
                    nc.vector.tensor_copy,
                )

                bias_all = keep.tile([P, GATES, H], BF16)
                for gate in range(0, GATES, 2):
                    both = spread_rows(nc, banks, ident_bf16, rows, (ROW_BIAS + gate, ROW_BIAS + gate + 1))
                    nc.scalar.copy(out=bias_all[:, gate : gate + 2, :], in_=both[:])

                assert X_CHUNKS == GATES
                x_codes = keep.tile([P, X_PASSES, BATCH], U32, align_bytes=64)
                x_scales = keep.tile([P, X_PASSES, BATCH], U8, align_bytes=64)
                zx = {}
                zh = {}
                rest = {}
                waiting = (h_grouped, h_codes[:], h_scales[:])
                for j in range(X_CHUNKS):
                    grouped = raw.tile([P, PASSES_PER_CHUNK, BATCH, PACK], BF16, tag="grouped", bufs=2, align_bytes=64)
                    words = [x_raw[j][:, m, :].bitcast(F32) for m in batch_tiles]
                    for g in range(PASSES_PER_CHUNK):
                        copy = nc.vector.tensor_copy if g % 2 == 0 else nc.scalar.copy
                        flip_pass(nc, banks, words, g, ident_f32, grouped[:, g], copy)
                        if g == 0:
                            quantise(nc, *waiting)
                    these = slice(PASSES_PER_CHUNK * j, PASSES_PER_CHUNK * (j + 1))
                    waiting = (grouped, x_codes[:, these, :], x_scales[:, these, :])

                    gate = j
                    for m in batch_tiles:
                        zx[gate, m] = late.tile([P, H], F32, name="zx%d_%d" % (gate, m))
                        nc.scalar.copy(out=units_as_pairs(zx[gate, m][:]), in_=units_in_order(expand("x", gate, m)[:]))
                        zh[gate, m] = late.tile([P, H], F32, name="zh%d_%d" % (gate, m))
                        nc.scalar.copy(out=units_as_pairs(zh[gate, m][:]), in_=units_in_order(expand("h", gate, m)[:]))
                        rest[gate, m] = late.tile([P, H], F32, name="rest%d_%d" % (gate, m))
                        nc.vector.tensor_tensor(
                            out=units_as_pairs(rest[gate, m][:]),
                            in0=units_in_order(expand("b", gate, m)[:]),
                            in1=units_as_pairs(bias_all[:, gate, :]),
                            op=ALU.add,
                        )

                quantise(nc, *waiting)

            for index in range(RING - X_CHUNKS, RING):
                load_weights(index)

            work = ctx.enter_context(tc.tile_pool(name="work", bufs=4, reuse_waits="tile"))
            acts = ctx.enter_context(tc.tile_pool(name="acts", bufs=1, reuse_waits="tile"))
        minus_rest_mean = {}

        def hidden_products():
            tiles = [(gate, m) for (gate,) in STAGES for m in batch_tiles]
            for gate, m in tiles:
                hh = banks.tile([P, H], F32, tag="bank")
                nc.tensor.matmul_mx(
                    out=hh[:],
                    lhsT=h_codes[:, 0, m * P : (m + 1) * P].bitcast(FP8X4),
                    lhsT_scale=h_scales[:, 0, m * P : (m + 1) * P],
                    rhs=whh[:, gate * H * PACK : (gate + 1) * H * PACK].bitcast(FP8X4),
                    rhs_scale=planes[:, PLANE_TILES, gate * H : (gate + 1) * H],
                    start=True,
                    stop=True,
                )
                nc.vector.tensor_tensor(out=zh[gate, m][:], in0=hh[:], in1=zh[gate, m][:], op=ALU.mult)
            for gate, m in tiles:
                rest_sum = stat.tile([P, 1], F32, tag="rest_sum")
                nc.vector.scalar_tensor_tensor(
                    out=rest[gate, m][:], in0=rest[gate, m][:], scalar=1.0, in1=zh[gate, m][:], op0=ALU.mult, op1=ALU.add,
                    accum_out=rest_sum[:],
                )
                minus_rest_mean[gate, m] = keep.tile([P, 1], F32, name="minus_rest_mean%d_%d" % (gate, m))
                nc.gpsimd.tensor_scalar(
                    out=minus_rest_mean[gate, m][:], in0=rest_sum[:], scalar1=-1.0 / H, scalar2=0.0, op0=ALU.mult, op1=ALU.add
                )

        ctx.enter_context(tc.manual_schedule(engines={mybir.EngineType.SP}))
        squashed = {}
        index = 0
        for gates in STAGES:
            if gates == STAGES[-3]:
                c_raw = keep.tile([P, M_TILES, H], BF16)
                nc.sync.dma_start(out=c_raw[:], in_=c.rearrange("(p m) k -> p m k", m=M_TILES))
            gamma_beta = {}
            xh = {}
            for gate in gates:
                gamma_beta[gate] = spread_rows(nc, banks, ident_bf16, rows, (ROW_GAMMA + gate, ROW_BETA + gate))
                for m in batch_tiles:
                    xh[gate, m] = banks.tile([P, H], F32, tag="bank", name="xh%d_%d" % (gate, m))
            if GATE_O in gates:
                cell_gamma_beta = spread_rows(nc, banks, ident_bf16, rows, (ROW_CELL_GAMMA, ROW_CELL_BETA))
            passes = SLOT_PASSES // len(gates)
            for first_pass in range(0, X_PASSES, passes):
                per_load = passes_per_load(index)
                for first in range(0, passes, per_load):
                    for position, gate in enumerate(gates):
                        for m in batch_tiles:
                            for i in range(first, first + per_load):
                                g = first_pass + i
                                nc.tensor.matmul_mx(
                                    out=xh[gate, m][:],
                                    lhsT=x_codes[:, g, m * P : (m + 1) * P].bitcast(FP8X4),
                                    lhsT_scale=x_scales[:, g, m * P : (m + 1) * P],
                                    rhs=w_loaded[index][:, i, position * H * PACK : (position + 1) * H * PACK].bitcast(FP8X4),
                                    rhs_scale=planes[
                                        4 * (g % PLANES_PER_TILE) : P, g // PLANES_PER_TILE, gate * H : (gate + 1) * H
                                    ],
                                    start=(g == 0),
                                    stop=(g == X_PASSES - 1),
                                )
                if index + RING < len(w_tiles):
                    load_weights(index + RING)
                index += 1
                if index == TILES_BEFORE_WHH:
                    hidden_products()

            for gate in gates:
                pre = [work.tile([P, H], F32, tag="pre", name="pre%d" % m) for m in batch_tiles]
                minus_mean = [stat.tile([P, 1], F32, tag="minus_mean", name="minus_mean%d" % m) for m in batch_tiles]
                for m in batch_tiles:
                    product_sum = stat.tile([P, 1], F32, tag="product_sum")
                    nc.vector.scalar_tensor_tensor(
                        out=pre[m][:], in0=xh[gate, m][:], scalar=1.0, in1=zx[gate, m][:], op0=ALU.mult, op1=ALU.mult,
                        accum_out=product_sum[:],
                    )
                    nc.scalar.activation(
                        out=minus_mean[m][:], in_=product_sum[:], func=ACT.Identity, scale=-1.0 / H,
                        bias=minus_rest_mean[gate, m][:],
                    )
                for m in batch_tiles:
                    nc.vector.tensor_tensor(out=pre[m][:], in0=pre[m][:], in1=rest[gate, m][:], op=ALU.add)
                halfway = [
                    norm_first_half(nc, work, stat, half, pre[m][:], minus_mean[m], gamma_beta[gate][:, 0, :])
                    for m in batch_tiles
                ]
                for m in batch_tiles:
                    centred, root = halfway[m]
                    inverse = norm_second_half(nc, stat, centred, root, gamma_beta[gate][:, 1, :])
                    squashed[gate, m] = acts.tile([P, H], F32, name="squashed%d_%d" % (gate, m))
                    nc.scalar.activation(
                        out=squashed[gate, m][:], in_=centred[:], func=(ACT.Tanh if gate == GATE_G else ACT.Sigmoid),
                        scale=inverse[:],
                    )

        cell = [squashed[GATE_I, m] for m in batch_tiles]
        minus_mean = [stat.tile([P, 1], F32, tag="minus_mean", name="minus_mean%d" % m) for m in batch_tiles]
        for m in batch_tiles:
            kept = squashed[GATE_F, m]
            nc.vector.tensor_tensor(out=kept[:], in0=kept[:], in1=c_raw[:, m, :], op=ALU.mult)
        for m in batch_tiles:
            nc.vector.tensor_tensor(out=cell[m][:], in0=cell[m][:], in1=squashed[GATE_G, m][:], op=ALU.mult)
        for m in batch_tiles:
            total = stat.tile([P, 1], F32, tag="total")
            nc.vector.scalar_tensor_tensor(
                out=cell[m][:], in0=cell[m][:], scalar=1.0, in1=squashed[GATE_F, m][:], op0=ALU.mult, op1=ALU.add,
                accum_out=total[:],
            )
            nc.scalar.mul(out=minus_mean[m][:], in_=total[:], mul=-1.0 / H)
        halfway = [
            norm_first_half(nc, work, stat, half, cell[m][:], minus_mean[m], cell_gamma_beta[:, 0, :]) for m in batch_tiles
        ]
        for m in batch_tiles:
            centred, root = halfway[m]
            inverse = norm_second_half(nc, stat, centred, root, cell_gamma_beta[:, 1, :])
            tanh_c = acts.tile([P, H], F32, name="tanh_c%d" % m)
            nc.scalar.activation(out=tanh_c[:], in_=centred[:], func=ACT.Tanh, scale=inverse[:])
            new_c = acts.tile([P, H], F32, name="new_c%d" % m)
            nc.scalar.activation(out=new_c[:], in_=centred[:], func=ACT.Copy, scale=inverse[:])
            nc.sync.dma_start(out=out_1.rearrange("(p m) n -> p m n", m=M_TILES)[:, m, :], in_=new_c[:])
            nc.vector.tensor_tensor(out=tanh_c[:], in0=tanh_c[:], in1=squashed[GATE_O, m][:], op=ALU.mult)
            nc.sync.dma_start(out=out_0.rearrange("(p m) n -> p m n", m=M_TILES)[:, m, :], in_=tanh_c[:])
